import numpy as np
import ml_dtypes


def mxq(x, axis, fmt="e4m3"):
    dtype, down = {"e4m3": (ml_dtypes.float8_e4m3fn, 7), "e5m2": (ml_dtypes.float8_e5m2, 14)}[fmt]
    v = np.moveaxis(np.asarray(x, np.float32).astype(ml_dtypes.bfloat16).astype(np.float64), axis, -1)
    blocks = v.reshape(v.shape[:-1] + (-1, 32))
    amax = np.abs(blocks).max(-1, keepdims=True)
    byte = np.maximum(np.where(amax > 0, np.frexp(amax)[1] - 1 + 127, 0) - down, 1)
    scale = np.exp2(byte - 127.0)
    codes = (blocks / scale).astype(np.float32).astype(dtype).astype(np.float64)
    return np.moveaxis((codes * scale).reshape(v.shape), -1, axis)


WIDE = False


def mx_kscale(k):
    if not WIDE:
        return np.ones(k)
    levels = np.array([10, -10, 5, -5, 0])
    a = np.random.permutation(np.resize(levels, k // 512 * 4)).reshape(k // 512, 4)
    idx = np.arange(k)
    return np.exp2(a[idx // 512, idx % 128 // 32])


BF16 = ml_dtypes.bfloat16


def bf(x):
    return np.asarray(x, np.float32).astype(BF16)


def f64(x):
    return np.asarray(x).astype(np.float64)


B, S, A, O, H, L = 4096, 256, 128, 128, 1024, 128
K1 = S + A + O


def setup_inputs():
    s = mx_kscale(K1)
    t = mx_kscale(H)
    w2 = np.random.standard_normal((H, 2 * L))
    w2 = np.concatenate([w2[:, :L] * 0.7 / np.sqrt(H), np.abs(w2[:, L:]) * 3.0 / H], axis=1)
    return {"prev_state": bf(np.random.standard_normal((B, S)) * s[:S]),
            "prev_action": bf(np.random.standard_normal((B, A)) * s[S:S + A]),
            "observation": bf(np.random.standard_normal((B, O)) * s[S + A:]),
            "eps": bf(np.random.standard_normal((B, L))),
            "rep_W1": bf(np.random.standard_normal((K1, H)) / np.sqrt(K1) / s[:, None] * t),
            "rep_b1": bf(np.random.standard_normal(H) * 0.1 * t),
            "rep_W2": bf(w2 / t[:, None]),
            "rep_b2": bf(np.concatenate([0.1 * np.random.standard_normal(L), 1.0 + 0.1 * np.random.standard_normal(L)]))}


def reference(prev_state, prev_action, observation, eps, rep_W1, rep_b1, rep_W2, rep_b2):
    x = np.concatenate([f64(prev_state), f64(prev_action), f64(observation)], axis=-1)
    h1 = np.maximum((mxq(x, 1, "e4m3") @ mxq(f64(rep_W1), 0, "e4m3")) + f64(rep_b1), 0.0)
    out = (mxq(h1, 1, "e4m3") @ mxq(f64(rep_W2), 0, "e4m3")) + f64(rep_b2)
    mean, std = np.split(out, 2, axis=-1)
    sample = mean + np.sqrt(std) * f64(eps)
    return mean, std, sample

@@ -1,0 +1,234 @@
+from contextlib import ExitStack
+
+import concourse.mybir as mybir
+from concourse.masks import make_identity
+
+F32 = mybir.dt.float32
+BF16 = mybir.dt.bfloat16
+U32 = mybir.dt.uint32
+U8 = mybir.dt.uint8
+FP8X4 = mybir.dt.float8_e4m3fn_x4
+ACT = mybir.ActivationFunctionType
+ALU = mybir.AluOpType
+
+P = 128
+PACK = 4
+K_PASS = P * PACK
+
+BATCH = 4096
+STATE = 256
+ACTION = 128
+OBS = 128
+K1 = STATE + ACTION + OBS
+HIDDEN = 1024
+LATENT = 128
+OUT = 2 * LATENT
+
+PASSES2 = HIDDEN // K_PASS
+H_TILES = HIDDEN // P
+SLOTS = BATCH // P
+CHUNK_SLOTS = 4
+CHUNK_ROWS = CHUNK_SLOTS * P
+CHUNKS = SLOTS // CHUNK_SLOTS
+BANK_SLOTS = 2
+WORD_HALVES = 2
+
+FLOPS = 2 * BATCH * K1 * HIDDEN + 2 * BATCH * HIDDEN * OUT
+
+
+def tile_rssm_pa_t_kernel(
+    tc,
+    prev_state,
+    prev_action,
+    observation,
+    eps,
+    rep_W1,
+    rep_b1,
+    rep_W2,
+    rep_b2,
+    mean_out,
+    std_out,
+    sample_out,
+):
+    nc = tc.nc
+    with ExitStack() as stack:
+        keep = stack.enter_context(tc.tile_pool(name="keep", bufs=1))
+        inputs = stack.enter_context(tc.tile_pool(name="inputs", bufs=CHUNKS))
+        work = stack.enter_context(tc.tile_pool(name="work", bufs=3))
+        psum_x = stack.enter_context(tc.psum_pool(name="psum_x", bufs=2))
+        psum_h = stack.enter_context(tc.psum_pool(name="psum_h", bufs=4))
+        psum_o = stack.enter_context(tc.psum_pool(name="psum_o", bufs=2))
+
+        w1_rows = keep.tile([P, PACK, HIDDEN], BF16)
+        w1_view = rep_W1.rearrange("(p j) h -> p j h", j=PACK)
+        for g in range(PASSES2):
+            h_cols = slice(g * K_PASS, (g + 1) * K_PASS)
+            nc.scalar.dma_start(out=w1_rows[:, :, h_cols], in_=w1_view[:, :, h_cols])
+        b1_bf16 = keep.tile([P, PASSES2, PACK], BF16)
+        nc.scalar.dma_start(
+            out=b1_bf16[:], in_=rep_b1.rearrange("(g m t) -> m g t", g=PASSES2, t=PACK)
+        )
+        w2_rows = keep.tile([P, PASSES2, PACK, OUT], BF16)
+        nc.scalar.dma_start(
+            out=w2_rows[:], in_=rep_W2.rearrange("(g p j) c -> p g j c", g=PASSES2, j=PACK)
+        )
+        b2_all = keep.tile([P, OUT], BF16)
+        nc.scalar.dma_start(out=b2_all[:], in_=rep_b2.partition_broadcast(P))
+
+        state_view = prev_state.rearrange("(p i) k -> p i k", i=SLOTS)
+        action_view = prev_action.rearrange("(p i) k -> p i k", i=SLOTS)
+        obs_view = observation.rearrange("(p i) k -> p i k", i=SLOTS)
+        eps_view = eps.rearrange("(p i) c -> p i c", i=SLOTS)
+        x_chunks = []
+        eps_chunks = []
+        for c in range(CHUNKS):
+            slots = slice(c * CHUNK_SLOTS, (c + 1) * CHUNK_SLOTS)
+            x_rows = inputs.tile([P, CHUNK_SLOTS, K1], BF16, name="x_rows")
+            nc.sync.dma_start(out=x_rows[:, :, 0:STATE], in_=state_view[:, slots, :])
+            nc.sync.dma_start(
+                out=x_rows[:, :, STATE : STATE + ACTION], in_=action_view[:, slots, :]
+            )
+            nc.sync.dma_start(out=x_rows[:, :, STATE + ACTION : K1], in_=obs_view[:, slots, :])
+            eps_rows = inputs.tile([P, CHUNK_SLOTS, LATENT], BF16, name="eps_rows")
+            nc.sync.dma_start(out=eps_rows[:], in_=eps_view[:, slots, :])
+            x_chunks.append(x_rows)
+            eps_chunks.append(eps_rows)
+
+        identity = keep.tile([P, P], F32)
+        make_identity(nc, identity[:])
+        one = keep.tile([P, 1], F32)
+        nc.vector.memset(one[:], 1.0)
+        nc.scalar.activation(out=one[:], in_=one[:], func=ACT.Sqrt)
+        b1 = keep.tile([P, H_TILES], F32)
+        nc.vector.tensor_copy(out=b1[:], in_=b1_bf16[:].rearrange("m g t -> m (g t)"))
+
+        w1_grouped = keep.tile([P, HIDDEN, PACK], BF16, align_bytes=64)
+        w1_codes = keep.tile([P, HIDDEN], U32, align_bytes=64)
+        w1_scales = keep.tile([P, HIDDEN], U8, align_bytes=64)
+        for g in range(PASSES2):
+            h_cols = slice(g * K_PASS, (g + 1) * K_PASS)
+            nc.vector.tensor_copy(
+                out=w1_grouped[:, h_cols, :].rearrange("p (t m) j -> p t m j", t=PACK),
+                in_=w1_rows[:, :, h_cols].rearrange("p j (m t) -> p t m j", t=PACK),
+            )
+            nc.vector.quantize_mx(
+                out=w1_codes[:, h_cols].bitcast(FP8X4),
+                scales=w1_scales[:, h_cols],
+                in_=w1_grouped[:, h_cols, :].rearrange("p h j -> p (h j)"),
+            )
+
+        w2_grouped = keep.tile([P, PASSES2, OUT, PACK], BF16, align_bytes=64)
+        w2_codes = keep.tile([P, PASSES2, OUT], U32, align_bytes=64)
+        w2_scales = keep.tile([P, PASSES2, OUT], U8, align_bytes=64)
+        nc.vector.tensor_copy(out=w2_grouped[:], in_=w2_rows[:].rearrange("p g j c -> p g c j"))
+        nc.vector.quantize_mx(
+            out=w2_codes[:].rearrange("p g c -> p (g c)").bitcast(FP8X4),
+            scales=w2_scales[:].rearrange("p g c -> p (g c)"),
+            in_=w2_grouped[:].rearrange("p g c j -> p (g c j)"),
+        )
+
+        b2_pairs = (
+            b2_all[:]
+            .rearrange("p (half c) -> p half c", half=2)
+            .unsqueeze(1)
+            .to_broadcast([P, BANK_SLOTS, 2, LATENT])
+        )
+        mean_view = mean_out.rearrange("(p i) c -> p i c", i=SLOTS)
+        std_view = std_out.rearrange("(p i) c -> p i c", i=SLOTS)
+        sample_view = sample_out.rearrange("(p i) c -> p i c", i=SLOTS)
+
+        for c in range(CHUNKS):
+            slots = slice(c * CHUNK_SLOTS, (c + 1) * CHUNK_SLOTS)
+
+            x_words = x_chunks[c][:].bitcast(F32).rearrange("p i (q u) -> p i u q", u=WORD_HALVES)
+            x_grouped = work.tile([P, CHUNK_ROWS * PACK], BF16, align_bytes=64)
+            x_grouped_words = (
+                x_grouped[:]
+                .bitcast(F32)
+                .rearrange("q (i b u) -> q i b u", i=CHUNK_SLOTS, u=WORD_HALVES)
+            )
+            for first in range(0, CHUNK_SLOTS, BANK_SLOTS):
+                x_t = psum_x.tile([P, BANK_SLOTS, WORD_HALVES, P], F32)
+                for i in range(BANK_SLOTS):
+                    for u in range(WORD_HALVES):
+                        nc.tensor.transpose(x_t[:, i, u, :], x_words[:, first + i, u, :], identity[:])
+                nc.scalar.copy(
+                    out=x_grouped_words[:, first : first + BANK_SLOTS],
+                    in_=x_t[:].rearrange("q i u b -> q i b u"),
+                )
+            x_codes = work.tile([P, CHUNK_ROWS], U32, align_bytes=64)
+            x_scales = work.tile([P, CHUNK_ROWS], U8, align_bytes=64)
+            nc.vector.quantize_mx(
+                out=x_codes[:].bitcast(FP8X4), scales=x_scales[:], in_=x_grouped[:]
+            )
+
+            h_tiles = work.tile([P, H_TILES, CHUNK_ROWS], BF16)
+            for tile_index in range(H_TILES):
+                m_cols = slice(tile_index * P, (tile_index + 1) * P)
+                h_acc = psum_h.tile([P, CHUNK_ROWS], F32)
+                nc.tensor.matmul_mx(
+                    out=h_acc[:],
+                    lhsT=w1_codes[:, m_cols].bitcast(FP8X4),
+                    lhsT_scale=w1_scales[:, m_cols],
+                    rhs=x_codes[:].bitcast(FP8X4),
+                    rhs_scale=x_scales[:],
+                    start=True,
+                    stop=True,
+                )
+                nc.scalar.activation(
+                    out=h_tiles[:, tile_index, :],
+                    in_=h_acc[:],
+                    func=ACT.Relu,
+                    bias=b1[:, tile_index : tile_index + 1],
+                    scale=1.0,
+                )
+
+            h_grouped = work.tile([P, PASSES2, CHUNK_ROWS, PACK], BF16, align_bytes=64)
+            for g in range(PASSES2):
+                nc.vector.tensor_copy(
+                    out=h_grouped[:, g].rearrange("m (r n) t -> m r t n", n=4),
+                    in_=h_tiles[:, g * PACK : (g + 1) * PACK, :].rearrange(
+                        "m t (r n) -> m r t n", n=4
+                    ),
+                )
+            h_codes = work.tile([P, PASSES2, CHUNK_ROWS], U32, align_bytes=64)
+            h_scales = work.tile([P, PASSES2, CHUNK_ROWS], U8, align_bytes=64)
+            nc.vector.quantize_mx(
+                out=h_codes[:].rearrange("m g b -> m (g b)").bitcast(FP8X4),
+                scales=h_scales[:].rearrange("m g b -> m (g b)"),
+                in_=h_grouped[:].rearrange("m g b t -> m (g b t)"),
+            )
+
+            mean_std = work.tile([P, 2, CHUNK_SLOTS, LATENT], F32)
+            for first in range(0, CHUNK_SLOTS, BANK_SLOTS):
+                o_acc = psum_o.tile([P, BANK_SLOTS, OUT], F32)
+                for i in range(BANK_SLOTS):
+                    b_cols = slice((first + i) * P, (first + i + 1) * P)
+                    for g in range(PASSES2):
+                        nc.tensor.matmul_mx(
+                            out=o_acc[:, i, :],
+                            lhsT=h_codes[:, g, b_cols].bitcast(FP8X4),
+                            lhsT_scale=h_scales[:, g, b_cols],
+                            rhs=w2_codes[:, g, :].bitcast(FP8X4),
+                            rhs_scale=w2_scales[:, g, :],
+                            start=(g == 0),
+                            stop=(g == PASSES2 - 1),
+                        )
+                nc.vector.tensor_tensor(
+                    out=mean_std[:, :, first : first + BANK_SLOTS, :].rearrange(
+                        "p half i c -> p i half c"
+                    ),
+                    in0=o_acc[:].rearrange("p i (half c) -> p i half c", half=2),
+                    in1=b2_pairs,
+                    op=ALU.add,
+                )
+
+            root = work.tile([P, CHUNK_SLOTS, LATENT], F32)
+            nc.scalar.activation(out=root[:], in_=mean_std[:, 1], func=ACT.Sqrt)
+            sample = work.tile([P, CHUNK_SLOTS, LATENT], F32)
+            nc.vector.tensor_tensor(out=sample[:], in0=root[:], in1=eps_chunks[c][:], op=ALU.mult)
+            nc.vector.tensor_tensor(out=sample[:], in0=sample[:], in1=mean_std[:, 0], op=ALU.add)
+
+            nc.sync.dma_start(out=mean_view[:, slots, :], in_=mean_std[:, 0])
+            nc.sync.dma_start(out=std_view[:, slots, :], in_=mean_std[:, 1])
+            nc.sync.dma_start(out=sample_view[:, slots, :], in_=sample[:])

@@ -25,12 +25,11 @@ LATENT = 128
 OUT = 2 * LATENT
 
 PASSES2 = HIDDEN // K_PASS
-H_TILES = HIDDEN // P
 SLOTS = BATCH // P
+BANK_SLOTS = 2
 CHUNK_SLOTS = 4
 CHUNK_ROWS = CHUNK_SLOTS * P
 CHUNKS = SLOTS // CHUNK_SLOTS
-BANK_SLOTS = 2
 WORD_HALVES = 2
 
 FLOPS = 2 * BATCH * K1 * HIDDEN + 2 * BATCH * HIDDEN * OUT
@@ -52,6 +51,7 @@ def tile_rssm_pa_t_kernel(
 ):
     nc = tc.nc
     with ExitStack() as stack:
+        stack.enter_context(tc.manual_schedule())
         keep = stack.enter_context(tc.tile_pool(name="keep", bufs=1))
         inputs = stack.enter_context(tc.tile_pool(name="inputs", bufs=CHUNKS))
         work = stack.enter_context(tc.tile_pool(name="work", bufs=3))
@@ -72,75 +72,89 @@ def tile_rssm_pa_t_kernel(
         nc.scalar.dma_start(
             out=w2_rows[:], in_=rep_W2.rearrange("(g p j) c -> p g j c", g=PASSES2, j=PACK)
         )
-        b2_all = keep.tile([P, OUT], BF16)
-        nc.scalar.dma_start(out=b2_all[:], in_=rep_b2.partition_broadcast(P))
+        b2_row = keep.tile([P, OUT], BF16)
+        nc.vector.memset(b2_row[:], 0.0)
+        nc.scalar.dma_start(out=b2_row[0:1, :], in_=rep_b2.rearrange("(o c) -> o c", o=1))
 
         state_view = prev_state.rearrange("(p i) k -> p i k", i=SLOTS)
         action_view = prev_action.rearrange("(p i) k -> p i k", i=SLOTS)
         obs_view = observation.rearrange("(p i) k -> p i k", i=SLOTS)
         eps_view = eps.rearrange("(p i) c -> p i c", i=SLOTS)
-        x_chunks = []
-        eps_chunks = []
+        x_rows = {}
+        eps_rows = {}
         for c in range(CHUNKS):
             slots = slice(c * CHUNK_SLOTS, (c + 1) * CHUNK_SLOTS)
-            x_rows = inputs.tile([P, CHUNK_SLOTS, K1], BF16, name="x_rows")
-            nc.sync.dma_start(out=x_rows[:, :, 0:STATE], in_=state_view[:, slots, :])
+            x_rows[c] = inputs.tile([P, CHUNK_SLOTS, K1], BF16, name="x_rows")
+            nc.sync.dma_start(out=x_rows[c][:, :, 0:STATE], in_=state_view[:, slots, :])
             nc.sync.dma_start(
-                out=x_rows[:, :, STATE : STATE + ACTION], in_=action_view[:, slots, :]
+                out=x_rows[c][:, :, STATE : STATE + ACTION], in_=action_view[:, slots, :]
             )
-            nc.sync.dma_start(out=x_rows[:, :, STATE + ACTION : K1], in_=obs_view[:, slots, :])
-            eps_rows = inputs.tile([P, CHUNK_SLOTS, LATENT], BF16, name="eps_rows")
-            nc.sync.dma_start(out=eps_rows[:], in_=eps_view[:, slots, :])
-            x_chunks.append(x_rows)
-            eps_chunks.append(eps_rows)
+            nc.sync.dma_start(out=x_rows[c][:, :, STATE + ACTION : K1], in_=obs_view[:, slots, :])
+            eps_rows[c] = inputs.tile([P, CHUNK_SLOTS, LATENT], BF16, name="eps_rows")
+            nc.sync.dma_start(out=eps_rows[c][:], in_=eps_view[:, slots, :])
 
-        identity = keep.tile([P, P], F32)
-        make_identity(nc, identity[:])
-        one = keep.tile([P, 1], F32)
-        nc.vector.memset(one[:], 1.0)
-        nc.scalar.activation(out=one[:], in_=one[:], func=ACT.Sqrt)
-        b1 = keep.tile([P, H_TILES], F32)
-        nc.vector.tensor_copy(out=b1[:], in_=b1_bf16[:].rearrange("m g t -> m (g t)"))
-
-        w1_grouped = keep.tile([P, HIDDEN, PACK], BF16, align_bytes=64)
-        w1_codes = keep.tile([P, HIDDEN], U32, align_bytes=64)
-        w1_scales = keep.tile([P, HIDDEN], U8, align_bytes=64)
-        for g in range(PASSES2):
-            h_cols = slice(g * K_PASS, (g + 1) * K_PASS)
-            nc.vector.tensor_copy(
-                out=w1_grouped[:, h_cols, :].rearrange("p (t m) j -> p t m j", t=PACK),
-                in_=w1_rows[:, :, h_cols].rearrange("p j (m t) -> p t m j", t=PACK),
-            )
-            nc.vector.quantize_mx(
-                out=w1_codes[:, h_cols].bitcast(FP8X4),
-                scales=w1_scales[:, h_cols],
-                in_=w1_grouped[:, h_cols, :].rearrange("p h j -> p (h j)"),
-            )
-
-        w2_grouped = keep.tile([P, PASSES2, OUT, PACK], BF16, align_bytes=64)
-        w2_codes = keep.tile([P, PASSES2, OUT], U32, align_bytes=64)
-        w2_scales = keep.tile([P, PASSES2, OUT], U8, align_bytes=64)
-        nc.vector.tensor_copy(out=w2_grouped[:], in_=w2_rows[:].rearrange("p g j c -> p g c j"))
-        nc.vector.quantize_mx(
-            out=w2_codes[:].rearrange("p g c -> p (g c)").bitcast(FP8X4),
-            scales=w2_scales[:].rearrange("p g c -> p (g c)"),
-            in_=w2_grouped[:].rearrange("p g c j -> p (g c j)"),
-        )
-
-        b2_pairs = (
-            b2_all[:]
-            .rearrange("p (half c) -> p half c", half=2)
-            .unsqueeze(1)
-            .to_broadcast([P, BANK_SLOTS, 2, LATENT])
-        )
         mean_view = mean_out.rearrange("(p i) c -> p i c", i=SLOTS)
         std_view = std_out.rearrange("(p i) c -> p i c", i=SLOTS)
         sample_view = sample_out.rearrange("(p i) c -> p i c", i=SLOTS)
 
-        for c in range(CHUNKS):
-            slots = slice(c * CHUNK_SLOTS, (c + 1) * CHUNK_SLOTS)
+        identity = keep.tile([P, P], F32)
+        make_identity(nc, identity[:])
+        ones = keep.tile([P, P], BF16)
+        nc.vector.memset(ones[:], 1.0)
+        one = keep.tile([P, 1], F32)
+        nc.vector.memset(one[:], 1.0)
+        nc.scalar.activation(out=one[:], in_=one[:], func=ACT.Sqrt)
 
-            x_words = x_chunks[c][:].bitcast(F32).rearrange("p i (q u) -> p i u q", u=WORD_HALVES)
+        w1_grouped = keep.tile([P, HIDDEN, PACK], BF16, align_bytes=64)
+        w1_codes = keep.tile([P, HIDDEN], U32, align_bytes=64)
+        w1_scales = keep.tile([P, HIDDEN], U8, align_bytes=64)
+        b1 = keep.tile([P, PASSES2 * PACK], F32)
+        w2_grouped = keep.tile([P, PASSES2, OUT, PACK], BF16, align_bytes=64)
+        w2_codes = keep.tile([P, PASSES2, OUT], U32, align_bytes=64)
+        w2_scales = keep.tile([P, PASSES2, OUT], U8, align_bytes=64)
+        b2_all = keep.tile([P, OUT], F32)
+
+        def quantise_w1():
+            for g in range(PASSES2):
+                h_cols = slice(g * K_PASS, (g + 1) * K_PASS)
+                nc.vector.tensor_copy(
+                    out=w1_grouped[:, h_cols, :].rearrange("p (t m) j -> p t m j", t=PACK),
+                    in_=w1_rows[:, :, h_cols].rearrange("p j (m t) -> p t m j", t=PACK),
+                )
+            nc.vector.tensor_copy(out=b1[:], in_=b1_bf16[:].rearrange("m g t -> m (g t)"))
+            for g in range(PASSES2):
+                h_cols = slice(g * K_PASS, (g + 1) * K_PASS)
+                nc.vector.quantize_mx(
+                    out=w1_codes[:, h_cols].bitcast(FP8X4),
+                    scales=w1_scales[:, h_cols],
+                    in_=w1_grouped[:, h_cols, :].rearrange("p h j -> p (h j)"),
+                )
+
+        def quantise_w2_and_spread_b2():
+            nc.vector.tensor_copy(
+                out=w2_grouped[:], in_=w2_rows[:].rearrange("p g j c -> p g c j")
+            )
+            b2_acc = psum_o.tile([P, BANK_SLOTS, OUT], F32, name="o_acc")
+            nc.tensor.matmul(out=b2_acc[:, 0, :], lhsT=ones[:], rhs=b2_row[:], start=True, stop=True)
+            nc.vector.tensor_copy(out=b2_all[:], in_=b2_acc[:, 0, :])
+            nc.vector.quantize_mx(
+                out=w2_codes[:].rearrange("p g c -> p (g c)").bitcast(FP8X4),
+                scales=w2_scales[:].rearrange("p g c -> p (g c)"),
+                in_=w2_grouped[:].rearrange("p g c j -> p (g c j)"),
+            )
+
+        x_codes = {}
+        x_scales = {}
+        h_tiles = {}
+        h_grouped = {}
+        h_codes = {}
+        h_scales = {}
+        mean_std = {}
+        root = {}
+        sample = {}
+
+        def transpose_and_quantise_x(c):
+            x_words = x_rows[c][:].bitcast(F32).rearrange("p i (q u) -> p i u q", u=WORD_HALVES)
             x_grouped = work.tile([P, CHUNK_ROWS * PACK], BF16, align_bytes=64)
             x_grouped_words = (
                 x_grouped[:]
@@ -156,50 +170,56 @@ def tile_rssm_pa_t_kernel(
                     out=x_grouped_words[:, first : first + BANK_SLOTS],
                     in_=x_t[:].rearrange("q i u b -> q i b u"),
                 )
-            x_codes = work.tile([P, CHUNK_ROWS], U32, align_bytes=64)
-            x_scales = work.tile([P, CHUNK_ROWS], U8, align_bytes=64)
+            x_codes[c] = work.tile([P, CHUNK_ROWS], U32, align_bytes=64, name="x_codes")
+            x_scales[c] = work.tile([P, CHUNK_ROWS], U8, align_bytes=64, name="x_scales")
             nc.vector.quantize_mx(
-                out=x_codes[:].bitcast(FP8X4), scales=x_scales[:], in_=x_grouped[:]
+                out=x_codes[c][:].bitcast(FP8X4), scales=x_scales[c][:], in_=x_grouped[:]
             )
 
-            h_tiles = work.tile([P, H_TILES, CHUNK_ROWS], BF16)
-            for tile_index in range(H_TILES):
-                m_cols = slice(tile_index * P, (tile_index + 1) * P)
+        def layer1(c, g):
+            h_tiles[c, g] = work.tile([P, PACK, CHUNK_ROWS], BF16, name="h_tiles", bufs=4)
+            for t in range(PACK):
+                m_cols = slice((g * PACK + t) * P, (g * PACK + t + 1) * P)
                 h_acc = psum_h.tile([P, CHUNK_ROWS], F32)
                 nc.tensor.matmul_mx(
                     out=h_acc[:],
                     lhsT=w1_codes[:, m_cols].bitcast(FP8X4),
                     lhsT_scale=w1_scales[:, m_cols],
-                    rhs=x_codes[:].bitcast(FP8X4),
-                    rhs_scale=x_scales[:],
+                    rhs=x_codes[c][:].bitcast(FP8X4),
+                    rhs_scale=x_scales[c][:],
                     start=True,
                     stop=True,
                 )
                 nc.scalar.activation(
-                    out=h_tiles[:, tile_index, :],
+                    out=h_tiles[c, g][:, t, :],
                     in_=h_acc[:],
                     func=ACT.Relu,
-                    bias=b1[:, tile_index : tile_index + 1],
+                    bias=b1[:, g * PACK + t : g * PACK + t + 1],
                     scale=1.0,
                 )
 
-            h_grouped = work.tile([P, PASSES2, CHUNK_ROWS, PACK], BF16, align_bytes=64)
-            for g in range(PASSES2):
-                nc.vector.tensor_copy(
-                    out=h_grouped[:, g].rearrange("m (r n) t -> m r t n", n=4),
-                    in_=h_tiles[:, g * PACK : (g + 1) * PACK, :].rearrange(
-                        "m t (r n) -> m r t n", n=4
-                    ),
+        def regroup_h(c, g):
+            if g == 0:
+                h_grouped[c] = work.tile(
+                    [P, PASSES2, CHUNK_ROWS, PACK], BF16, align_bytes=64, name="h_grouped"
                 )
-            h_codes = work.tile([P, PASSES2, CHUNK_ROWS], U32, align_bytes=64)
-            h_scales = work.tile([P, PASSES2, CHUNK_ROWS], U8, align_bytes=64)
-            nc.vector.quantize_mx(
-                out=h_codes[:].rearrange("m g b -> m (g b)").bitcast(FP8X4),
-                scales=h_scales[:].rearrange("m g b -> m (g b)"),
-                in_=h_grouped[:].rearrange("m g b t -> m (g b t)"),
+            nc.vector.tensor_copy(
+                out=h_grouped[c][:, g].rearrange("m (r n) t -> m r t n", n=4),
+                in_=h_tiles[c, g][:].rearrange("m t (r n) -> m r t n", n=4),
             )
 
-            mean_std = work.tile([P, 2, CHUNK_SLOTS, LATENT], F32)
+        def quantise_h(c):
+            h_codes[c] = work.tile([P, PASSES2, CHUNK_ROWS], U32, align_bytes=64, name="h_codes")
+            h_scales[c] = work.tile([P, PASSES2, CHUNK_ROWS], U8, align_bytes=64, name="h_scales")
+            nc.vector.quantize_mx(
+                out=h_codes[c][:].rearrange("m g b -> m (g b)").bitcast(FP8X4),
+                scales=h_scales[c][:].rearrange("m g b -> m (g b)"),
+                in_=h_grouped[c][:].rearrange("m g b t -> m (g b t)"),
+            )
+
+        def layer2(c):
+            slots = slice(c * CHUNK_SLOTS, (c + 1) * CHUNK_SLOTS)
+            mean_std[c] = work.tile([P, 2, CHUNK_SLOTS, LATENT], F32, name="mean_std")
             for first in range(0, CHUNK_SLOTS, BANK_SLOTS):
                 o_acc = psum_o.tile([P, BANK_SLOTS, OUT], F32)
                 for i in range(BANK_SLOTS):
@@ -207,28 +227,65 @@ def tile_rssm_pa_t_kernel(
                     for g in range(PASSES2):
                         nc.tensor.matmul_mx(
                             out=o_acc[:, i, :],
-                            lhsT=h_codes[:, g, b_cols].bitcast(FP8X4),
-                            lhsT_scale=h_scales[:, g, b_cols],
+                            lhsT=h_codes[c][:, g, b_cols].bitcast(FP8X4),
+                            lhsT_scale=h_scales[c][:, g, b_cols],
                             rhs=w2_codes[:, g, :].bitcast(FP8X4),
                             rhs_scale=w2_scales[:, g, :],
                             start=(g == 0),
                             stop=(g == PASSES2 - 1),
                         )
                 nc.vector.tensor_tensor(
-                    out=mean_std[:, :, first : first + BANK_SLOTS, :].rearrange(
+                    out=mean_std[c][:, :, first : first + BANK_SLOTS, :].rearrange(
                         "p half i c -> p i half c"
                     ),
                     in0=o_acc[:].rearrange("p i (half c) -> p i half c", half=2),
-                    in1=b2_pairs,
+                    in1=b2_all[:]
+                    .rearrange("p (half c) -> p half c", half=2)
+                    .unsqueeze(1)
+                    .to_broadcast([P, BANK_SLOTS, 2, LATENT]),
                     op=ALU.add,
                 )
+            root[c] = work.tile([P, CHUNK_SLOTS, LATENT], F32, name="root")
+            nc.scalar.activation(out=root[c][:], in_=mean_std[c][:, 1], func=ACT.Sqrt)
+            nc.sync.dma_start(out=mean_view[:, slots, :], in_=mean_std[c][:, 0])
+            nc.sync.dma_start(out=std_view[:, slots, :], in_=mean_std[c][:, 1])
 
-            root = work.tile([P, CHUNK_SLOTS, LATENT], F32)
-            nc.scalar.activation(out=root[:], in_=mean_std[:, 1], func=ACT.Sqrt)
-            sample = work.tile([P, CHUNK_SLOTS, LATENT], F32)
-            nc.vector.tensor_tensor(out=sample[:], in0=root[:], in1=eps_chunks[c][:], op=ALU.mult)
-            nc.vector.tensor_tensor(out=sample[:], in0=sample[:], in1=mean_std[:, 0], op=ALU.add)
+        def noise(c):
+            sample[c] = work.tile([P, CHUNK_SLOTS, LATENT], F32, name="sample")
+            nc.vector.tensor_tensor(
+                out=sample[c][:], in0=root[c][:], in1=eps_rows[c][:], op=ALU.mult
+            )
 
-            nc.sync.dma_start(out=mean_view[:, slots, :], in_=mean_std[:, 0])
-            nc.sync.dma_start(out=std_view[:, slots, :], in_=mean_std[:, 1])
-            nc.sync.dma_start(out=sample_view[:, slots, :], in_=sample[:])
+        def add_mean_and_store(c):
+            slots = slice(c * CHUNK_SLOTS, (c + 1) * CHUNK_SLOTS)
+            nc.vector.tensor_tensor(
+                out=sample[c][:], in0=sample[c][:], in1=mean_std[c][:, 0], op=ALU.add
+            )
+            nc.sync.dma_start(out=sample_view[:, slots, :], in_=sample[c][:])
+
+        quantise_w1()
+        transpose_and_quantise_x(0)
+        layer1(0, 0)
+        quantise_w2_and_spread_b2()
+        for n in range(CHUNKS + 1):
+            started = n + 1 < CHUNKS
+            running = n < CHUNKS
+            ending = n >= 1
+            if started:
+                transpose_and_quantise_x(n + 1)
+            if running:
+                layer1(n, 1)
+            if ending:
+                layer2(n - 1)
+            if running:
+                regroup_h(n, 0)
+            if started:
+                layer1(n + 1, 0)
+            if running:
+                regroup_h(n, 1)
+            if ending:
+                noise(n - 1)
+            if running:
+                quantise_h(n)
+            if ending:
+                add_mean_and_store(n - 1)

@@ -26,8 +26,7 @@ OUT = 2 * LATENT
 
 PASSES2 = HIDDEN // K_PASS
 SLOTS = BATCH // P
-BANK_SLOTS = 2
-CHUNK_SLOTS = 4
+CHUNK_SLOTS = 2
 CHUNK_ROWS = CHUNK_SLOTS * P
 CHUNKS = SLOTS // CHUNK_SLOTS
 WORD_HALVES = 2
@@ -54,20 +53,20 @@ def tile_rssm_pa_t_kernel(
         stack.enter_context(tc.manual_schedule())
         keep = stack.enter_context(tc.tile_pool(name="keep", bufs=1))
         inputs = stack.enter_context(tc.tile_pool(name="inputs", bufs=CHUNKS))
-        work = stack.enter_context(tc.tile_pool(name="work", bufs=3))
+        work = stack.enter_context(tc.tile_pool(name="work", bufs=6))
         psum_x = stack.enter_context(tc.psum_pool(name="psum_x", bufs=2))
         psum_h = stack.enter_context(tc.psum_pool(name="psum_h", bufs=4))
         psum_o = stack.enter_context(tc.psum_pool(name="psum_o", bufs=2))
 
         w1_rows = keep.tile([P, PACK, HIDDEN], BF16)
         w1_view = rep_W1.rearrange("(p j) h -> p j h", j=PACK)
-        for g in range(PASSES2):
-            h_cols = slice(g * K_PASS, (g + 1) * K_PASS)
-            nc.scalar.dma_start(out=w1_rows[:, :, h_cols], in_=w1_view[:, :, h_cols])
         b1_bf16 = keep.tile([P, PASSES2, PACK], BF16)
         nc.scalar.dma_start(
             out=b1_bf16[:], in_=rep_b1.rearrange("(g m t) -> m g t", g=PASSES2, t=PACK)
         )
+        for g in range(PASSES2):
+            h_cols = slice(g * K_PASS, (g + 1) * K_PASS)
+            nc.scalar.dma_start(out=w1_rows[:, :, h_cols], in_=w1_view[:, :, h_cols])
         w2_rows = keep.tile([P, PASSES2, PACK, OUT], BF16)
         nc.scalar.dma_start(
             out=w2_rows[:], in_=rep_W2.rearrange("(g p j) c -> p g j c", g=PASSES2, j=PACK)
@@ -114,27 +113,26 @@ def tile_rssm_pa_t_kernel(
         w2_scales = keep.tile([P, PASSES2, OUT], U8, align_bytes=64)
         b2_all = keep.tile([P, OUT], F32)
 
-        def quantise_w1():
-            for g in range(PASSES2):
-                h_cols = slice(g * K_PASS, (g + 1) * K_PASS)
-                nc.vector.tensor_copy(
-                    out=w1_grouped[:, h_cols, :].rearrange("p (t m) j -> p t m j", t=PACK),
-                    in_=w1_rows[:, :, h_cols].rearrange("p j (m t) -> p t m j", t=PACK),
-                )
-            nc.vector.tensor_copy(out=b1[:], in_=b1_bf16[:].rearrange("m g t -> m (g t)"))
-            for g in range(PASSES2):
-                h_cols = slice(g * K_PASS, (g + 1) * K_PASS)
-                nc.vector.quantize_mx(
-                    out=w1_codes[:, h_cols].bitcast(FP8X4),
-                    scales=w1_scales[:, h_cols],
-                    in_=w1_grouped[:, h_cols, :].rearrange("p h j -> p (h j)"),
-                )
+        def quantise_w1(g):
+            h_cols = slice(g * K_PASS, (g + 1) * K_PASS)
+            nc.vector.tensor_copy(
+                out=w1_grouped[:, h_cols, :].rearrange("p (t m) j -> p t m j", t=PACK),
+                in_=w1_rows[:, :, h_cols].rearrange("p j (m t) -> p t m j", t=PACK),
+            )
+            nc.vector.tensor_copy(
+                out=b1[:, g * PACK : (g + 1) * PACK], in_=b1_bf16[:, g, :]
+            )
+            nc.vector.quantize_mx(
+                out=w1_codes[:, h_cols].bitcast(FP8X4),
+                scales=w1_scales[:, h_cols],
+                in_=w1_grouped[:, h_cols, :].rearrange("p h j -> p (h j)"),
+            )
 
         def quantise_w2_and_spread_b2():
             nc.vector.tensor_copy(
                 out=w2_grouped[:], in_=w2_rows[:].rearrange("p g j c -> p g c j")
             )
-            b2_acc = psum_o.tile([P, BANK_SLOTS, OUT], F32, name="o_acc")
+            b2_acc = psum_o.tile([P, CHUNK_SLOTS, OUT], F32, name="o_acc")
             nc.tensor.matmul(out=b2_acc[:, 0, :], lhsT=ones[:], rhs=b2_row[:], start=True, stop=True)
             nc.vector.tensor_copy(out=b2_all[:], in_=b2_acc[:, 0, :])
             nc.vector.quantize_mx(
@@ -143,41 +141,46 @@ def tile_rssm_pa_t_kernel(
                 in_=w2_grouped[:].rearrange("p g c j -> p (g c j)"),
             )
 
+        x_t = {}
+        x_grouped = {}
         x_codes = {}
         x_scales = {}
         h_tiles = {}
         h_grouped = {}
         h_codes = {}
         h_scales = {}
+        o_acc = {}
         mean_std = {}
         root = {}
         sample = {}
 
-        def transpose_and_quantise_x(c):
+        def transpose_x(c):
             x_words = x_rows[c][:].bitcast(F32).rearrange("p i (q u) -> p i u q", u=WORD_HALVES)
-            x_grouped = work.tile([P, CHUNK_ROWS * PACK], BF16, align_bytes=64)
-            x_grouped_words = (
-                x_grouped[:]
-                .bitcast(F32)
-                .rearrange("q (i b u) -> q i b u", i=CHUNK_SLOTS, u=WORD_HALVES)
+            x_t[c] = psum_x.tile([P, CHUNK_SLOTS, WORD_HALVES, P], F32, name="x_t")
+            for i in range(CHUNK_SLOTS):
+                for u in range(WORD_HALVES):
+                    nc.tensor.transpose(x_t[c][:, i, u, :], x_words[:, i, u, :], identity[:])
+
+        def copy_x(c):
+            x_grouped[c] = work.tile(
+                [P, CHUNK_ROWS * PACK], BF16, align_bytes=64, name="x_grouped"
             )
-            for first in range(0, CHUNK_SLOTS, BANK_SLOTS):
-                x_t = psum_x.tile([P, BANK_SLOTS, WORD_HALVES, P], F32)
-                for i in range(BANK_SLOTS):
-                    for u in range(WORD_HALVES):
-                        nc.tensor.transpose(x_t[:, i, u, :], x_words[:, first + i, u, :], identity[:])
-                nc.scalar.copy(
-                    out=x_grouped_words[:, first : first + BANK_SLOTS],
-                    in_=x_t[:].rearrange("q i u b -> q i b u"),
-                )
+            nc.scalar.copy(
+                out=x_grouped[c][:]
+                .bitcast(F32)
+                .rearrange("q (i b u) -> q i b u", i=CHUNK_SLOTS, u=WORD_HALVES),
+                in_=x_t[c][:].rearrange("q i u b -> q i b u"),
+            )
+
+        def quantise_x(c):
             x_codes[c] = work.tile([P, CHUNK_ROWS], U32, align_bytes=64, name="x_codes")
             x_scales[c] = work.tile([P, CHUNK_ROWS], U8, align_bytes=64, name="x_scales")
             nc.vector.quantize_mx(
-                out=x_codes[c][:].bitcast(FP8X4), scales=x_scales[c][:], in_=x_grouped[:]
+                out=x_codes[c][:].bitcast(FP8X4), scales=x_scales[c][:], in_=x_grouped[c][:]
             )
 
         def layer1(c, g):
-            h_tiles[c, g] = work.tile([P, PACK, CHUNK_ROWS], BF16, name="h_tiles", bufs=4)
+            h_tiles[c, g] = work.tile([P, PACK, CHUNK_ROWS], BF16, name="h_tiles")
             for t in range(PACK):
                 m_cols = slice((g * PACK + t) * P, (g * PACK + t + 1) * P)
                 h_acc = psum_h.tile([P, CHUNK_ROWS], F32)
@@ -218,37 +221,38 @@ def tile_rssm_pa_t_kernel(
             )
 
         def layer2(c):
+            o_acc[c] = psum_o.tile([P, CHUNK_SLOTS, OUT], F32, name="o_acc")
+            for i in range(CHUNK_SLOTS):
+                b_cols = slice(i * P, (i + 1) * P)
+                for g in range(PASSES2):
+                    nc.tensor.matmul_mx(
+                        out=o_acc[c][:, i, :],
+                        lhsT=h_codes[c][:, g, b_cols].bitcast(FP8X4),
+                        lhsT_scale=h_scales[c][:, g, b_cols],
+                        rhs=w2_codes[:, g, :].bitcast(FP8X4),
+                        rhs_scale=w2_scales[:, g, :],
+                        start=(g == 0),
+                        stop=(g == PASSES2 - 1),
+                    )
+
+        def add_b2_and_store(c):
             slots = slice(c * CHUNK_SLOTS, (c + 1) * CHUNK_SLOTS)
             mean_std[c] = work.tile([P, 2, CHUNK_SLOTS, LATENT], F32, name="mean_std")
-            for first in range(0, CHUNK_SLOTS, BANK_SLOTS):
-                o_acc = psum_o.tile([P, BANK_SLOTS, OUT], F32)
-                for i in range(BANK_SLOTS):
-                    b_cols = slice((first + i) * P, (first + i + 1) * P)
-                    for g in range(PASSES2):
-                        nc.tensor.matmul_mx(
-                            out=o_acc[:, i, :],
-                            lhsT=h_codes[c][:, g, b_cols].bitcast(FP8X4),
-                            lhsT_scale=h_scales[c][:, g, b_cols],
-                            rhs=w2_codes[:, g, :].bitcast(FP8X4),
-                            rhs_scale=w2_scales[:, g, :],
-                            start=(g == 0),
-                            stop=(g == PASSES2 - 1),
-                        )
-                nc.vector.tensor_tensor(
-                    out=mean_std[c][:, :, first : first + BANK_SLOTS, :].rearrange(
-                        "p half i c -> p i half c"
-                    ),
-                    in0=o_acc[:].rearrange("p i (half c) -> p i half c", half=2),
-                    in1=b2_all[:]
-                    .rearrange("p (half c) -> p half c", half=2)
-                    .unsqueeze(1)
-                    .to_broadcast([P, BANK_SLOTS, 2, LATENT]),
-                    op=ALU.add,
-                )
-            root[c] = work.tile([P, CHUNK_SLOTS, LATENT], F32, name="root")
-            nc.scalar.activation(out=root[c][:], in_=mean_std[c][:, 1], func=ACT.Sqrt)
+            nc.vector.tensor_tensor(
+                out=mean_std[c][:].rearrange("p half i c -> p i half c"),
+                in0=o_acc[c][:].rearrange("p i (half c) -> p i half c", half=2),
+                in1=b2_all[:]
+                .rearrange("p (half c) -> p half c", half=2)
+                .unsqueeze(1)
+                .to_broadcast([P, CHUNK_SLOTS, 2, LATENT]),
+                op=ALU.add,
+            )
             nc.sync.dma_start(out=mean_view[:, slots, :], in_=mean_std[c][:, 0])
             nc.sync.dma_start(out=std_view[:, slots, :], in_=mean_std[c][:, 1])
+
+        def root_of_std(c):
+            root[c] = work.tile([P, CHUNK_SLOTS, LATENT], F32, name="root")
+            nc.scalar.activation(out=root[c][:], in_=mean_std[c][:, 1], func=ACT.Sqrt)
 
         def noise(c):
             sample[c] = work.tile([P, CHUNK_SLOTS, LATENT], F32, name="sample")
@@ -263,29 +267,43 @@ def tile_rssm_pa_t_kernel(
             )
             nc.sync.dma_start(out=sample_view[:, slots, :], in_=sample[c][:])
 
-        quantise_w1()
-        transpose_and_quantise_x(0)
+        def exists(c):
+            return 0 <= c < CHUNKS
+
+        transpose_x(0)
+        transpose_x(1)
+        quantise_w1(0)
+        copy_x(0)
+        quantise_x(0)
+        quantise_w1(1)
+        copy_x(1)
+        quantise_x(1)
         layer1(0, 0)
+        transpose_x(2)
         quantise_w2_and_spread_b2()
-        for n in range(CHUNKS + 1):
-            started = n + 1 < CHUNKS
-            running = n < CHUNKS
-            ending = n >= 1
-            if started:
-                transpose_and_quantise_x(n + 1)
-            if running:
+        for n in range(CHUNKS + 4):
+            if exists(n):
                 layer1(n, 1)
-            if ending:
-                layer2(n - 1)
-            if running:
                 regroup_h(n, 0)
-            if started:
-                layer1(n + 1, 0)
-            if running:
+            if exists(n - 4):
+                add_mean_and_store(n - 4)
+            if exists(n + 2):
+                copy_x(n + 2)
+            if exists(n - 2):
+                add_b2_and_store(n - 2)
+            if exists(n - 3):
+                root_of_std(n - 3)
+            if exists(n):
                 regroup_h(n, 1)
-            if ending:
-                noise(n - 1)
-            if running:
+            if exists(n + 1):
+                layer1(n + 1, 0)
+            if exists(n + 2):
+                quantise_x(n + 2)
+            if exists(n + 3):
+                transpose_x(n + 3)
+            if exists(n - 3):
+                noise(n - 3)
+            if exists(n - 1):
+                layer2(n - 1)
+            if exists(n):
                 quantise_h(n)
-            if ending:
-                add_mean_and_store(n - 1)

@@ -26,7 +26,8 @@ OUT = 2 * LATENT
 
 PASSES2 = HIDDEN // K_PASS
 SLOTS = BATCH // P
-CHUNK_SLOTS = 2
+CHUNK_SLOTS = 4
+BANK_SLOTS = 2
 CHUNK_ROWS = CHUNK_SLOTS * P
 CHUNKS = SLOTS // CHUNK_SLOTS
 WORD_HALVES = 2
@@ -53,35 +54,29 @@ def tile_rssm_pa_t_kernel(
         stack.enter_context(tc.manual_schedule())
         keep = stack.enter_context(tc.tile_pool(name="keep", bufs=1))
         inputs = stack.enter_context(tc.tile_pool(name="inputs", bufs=CHUNKS))
-        work = stack.enter_context(tc.tile_pool(name="work", bufs=6))
+        work = stack.enter_context(tc.tile_pool(name="work", bufs=4))
         psum_x = stack.enter_context(tc.psum_pool(name="psum_x", bufs=2))
         psum_h = stack.enter_context(tc.psum_pool(name="psum_h", bufs=4))
         psum_o = stack.enter_context(tc.psum_pool(name="psum_o", bufs=2))
 
         w1_rows = keep.tile([P, PACK, HIDDEN], BF16)
         w1_view = rep_W1.rearrange("(p j) h -> p j h", j=PACK)
-        b1_bf16 = keep.tile([P, PASSES2, PACK], BF16)
-        nc.scalar.dma_start(
-            out=b1_bf16[:], in_=rep_b1.rearrange("(g m t) -> m g t", g=PASSES2, t=PACK)
-        )
-        for g in range(PASSES2):
-            h_cols = slice(g * K_PASS, (g + 1) * K_PASS)
-            nc.scalar.dma_start(out=w1_rows[:, :, h_cols], in_=w1_view[:, :, h_cols])
+        b1 = keep.tile([P, PASSES2, PACK], BF16)
         w2_rows = keep.tile([P, PASSES2, PACK, OUT], BF16)
-        nc.scalar.dma_start(
-            out=w2_rows[:], in_=rep_W2.rearrange("(g p j) c -> p g j c", g=PASSES2, j=PACK)
-        )
         b2_row = keep.tile([P, OUT], BF16)
         nc.vector.memset(b2_row[:], 0.0)
-        nc.scalar.dma_start(out=b2_row[0:1, :], in_=rep_b2.rearrange("(o c) -> o c", o=1))
-
         state_view = prev_state.rearrange("(p i) k -> p i k", i=SLOTS)
         action_view = prev_action.rearrange("(p i) k -> p i k", i=SLOTS)
         obs_view = observation.rearrange("(p i) k -> p i k", i=SLOTS)
         eps_view = eps.rearrange("(p i) c -> p i c", i=SLOTS)
         x_rows = {}
         eps_rows = {}
-        for c in range(CHUNKS):
+
+        def load_w1(g):
+            h_cols = slice(g * K_PASS, (g + 1) * K_PASS)
+            nc.sync.dma_start(out=w1_rows[:, :, h_cols], in_=w1_view[:, :, h_cols])
+
+        def load_x(c):
             slots = slice(c * CHUNK_SLOTS, (c + 1) * CHUNK_SLOTS)
             x_rows[c] = inputs.tile([P, CHUNK_SLOTS, K1], BF16, name="x_rows")
             nc.sync.dma_start(out=x_rows[c][:, :, 0:STATE], in_=state_view[:, slots, :])
@@ -89,8 +84,26 @@ def tile_rssm_pa_t_kernel(
                 out=x_rows[c][:, :, STATE : STATE + ACTION], in_=action_view[:, slots, :]
             )
             nc.sync.dma_start(out=x_rows[c][:, :, STATE + ACTION : K1], in_=obs_view[:, slots, :])
+
+        def load_eps(c):
+            slots = slice(c * CHUNK_SLOTS, (c + 1) * CHUNK_SLOTS)
             eps_rows[c] = inputs.tile([P, CHUNK_SLOTS, LATENT], BF16, name="eps_rows")
             nc.sync.dma_start(out=eps_rows[c][:], in_=eps_view[:, slots, :])
+
+        load_w1(0)
+        load_x(0)
+        nc.sync.dma_start(out=b1[:], in_=rep_b1.rearrange("(g m t) -> m g t", g=PASSES2, t=PACK))
+        load_w1(1)
+        load_x(1)
+        nc.sync.dma_start(
+            out=w2_rows[:], in_=rep_W2.rearrange("(g p j) c -> p g j c", g=PASSES2, j=PACK)
+        )
+        nc.sync.dma_start(out=b2_row[0:1, :], in_=rep_b2.rearrange("(o c) -> o c", o=1))
+        for c in range(2, CHUNKS):
+            load_x(c)
+            load_eps(c - 2)
+        load_eps(CHUNKS - 2)
+        load_eps(CHUNKS - 1)
 
         mean_view = mean_out.rearrange("(p i) c -> p i c", i=SLOTS)
         std_view = std_out.rearrange("(p i) c -> p i c", i=SLOTS)
@@ -107,7 +120,6 @@ def tile_rssm_pa_t_kernel(
         w1_grouped = keep.tile([P, HIDDEN, PACK], BF16, align_bytes=64)
         w1_codes = keep.tile([P, HIDDEN], U32, align_bytes=64)
         w1_scales = keep.tile([P, HIDDEN], U8, align_bytes=64)
-        b1 = keep.tile([P, PASSES2 * PACK], F32)
         w2_grouped = keep.tile([P, PASSES2, OUT, PACK], BF16, align_bytes=64)
         w2_codes = keep.tile([P, PASSES2, OUT], U32, align_bytes=64)
         w2_scales = keep.tile([P, PASSES2, OUT], U8, align_bytes=64)
@@ -119,9 +131,6 @@ def tile_rssm_pa_t_kernel(
                 out=w1_grouped[:, h_cols, :].rearrange("p (t m) j -> p t m j", t=PACK),
                 in_=w1_rows[:, :, h_cols].rearrange("p j (m t) -> p t m j", t=PACK),
             )
-            nc.vector.tensor_copy(
-                out=b1[:, g * PACK : (g + 1) * PACK], in_=b1_bf16[:, g, :]
-            )
             nc.vector.quantize_mx(
                 out=w1_codes[:, h_cols].bitcast(FP8X4),
                 scales=w1_scales[:, h_cols],
@@ -132,7 +141,7 @@ def tile_rssm_pa_t_kernel(
             nc.vector.tensor_copy(
                 out=w2_grouped[:], in_=w2_rows[:].rearrange("p g j c -> p g c j")
             )
-            b2_acc = psum_o.tile([P, CHUNK_SLOTS, OUT], F32, name="o_acc")
+            b2_acc = psum_o.tile([P, BANK_SLOTS, OUT], F32, name="o_acc")
             nc.tensor.matmul(out=b2_acc[:, 0, :], lhsT=ones[:], rhs=b2_row[:], start=True, stop=True)
             nc.vector.tensor_copy(out=b2_all[:], in_=b2_acc[:, 0, :])
             nc.vector.quantize_mx(
@@ -156,21 +165,28 @@ def tile_rssm_pa_t_kernel(
 
         def transpose_x(c):
             x_words = x_rows[c][:].bitcast(F32).rearrange("p i (q u) -> p i u q", u=WORD_HALVES)
-            x_t[c] = psum_x.tile([P, CHUNK_SLOTS, WORD_HALVES, P], F32, name="x_t")
-            for i in range(CHUNK_SLOTS):
-                for u in range(WORD_HALVES):
-                    nc.tensor.transpose(x_t[c][:, i, u, :], x_words[:, i, u, :], identity[:])
+            for first in range(0, CHUNK_SLOTS, BANK_SLOTS):
+                x_t[c, first] = psum_x.tile([P, BANK_SLOTS, WORD_HALVES, P], F32, name="x_t")
+                for i in range(BANK_SLOTS):
+                    for u in range(WORD_HALVES):
+                        nc.tensor.transpose(
+                            x_t[c, first][:, i, u, :], x_words[:, first + i, u, :], identity[:]
+                        )
 
         def copy_x(c):
             x_grouped[c] = work.tile(
                 [P, CHUNK_ROWS * PACK], BF16, align_bytes=64, name="x_grouped"
             )
-            nc.scalar.copy(
-                out=x_grouped[c][:]
+            x_grouped_words = (
+                x_grouped[c][:]
                 .bitcast(F32)
-                .rearrange("q (i b u) -> q i b u", i=CHUNK_SLOTS, u=WORD_HALVES),
-                in_=x_t[c][:].rearrange("q i u b -> q i b u"),
+                .rearrange("q (i b u) -> q i b u", i=CHUNK_SLOTS, u=WORD_HALVES)
             )
+            for first in range(0, CHUNK_SLOTS, BANK_SLOTS):
+                nc.scalar.copy(
+                    out=x_grouped_words[:, first : first + BANK_SLOTS],
+                    in_=x_t[c, first][:].rearrange("q i u b -> q i b u"),
+                )
 
         def quantise_x(c):
             x_codes[c] = work.tile([P, CHUNK_ROWS], U32, align_bytes=64, name="x_codes")
@@ -197,7 +213,7 @@ def tile_rssm_pa_t_kernel(
                     out=h_tiles[c, g][:, t, :],
                     in_=h_acc[:],
                     func=ACT.Relu,
-                    bias=b1[:, g * PACK + t : g * PACK + t + 1],
+                    bias=b1[:, g, t : t + 1],
                     scale=1.0,
                 )
 
@@ -221,32 +237,36 @@ def tile_rssm_pa_t_kernel(
             )
 
         def layer2(c):
-            o_acc[c] = psum_o.tile([P, CHUNK_SLOTS, OUT], F32, name="o_acc")
-            for i in range(CHUNK_SLOTS):
-                b_cols = slice(i * P, (i + 1) * P)
-                for g in range(PASSES2):
-                    nc.tensor.matmul_mx(
-                        out=o_acc[c][:, i, :],
-                        lhsT=h_codes[c][:, g, b_cols].bitcast(FP8X4),
-                        lhsT_scale=h_scales[c][:, g, b_cols],
-                        rhs=w2_codes[:, g, :].bitcast(FP8X4),
-                        rhs_scale=w2_scales[:, g, :],
-                        start=(g == 0),
-                        stop=(g == PASSES2 - 1),
-                    )
+            for first in range(0, CHUNK_SLOTS, BANK_SLOTS):
+                o_acc[c, first] = psum_o.tile([P, BANK_SLOTS, OUT], F32, name="o_acc")
+                for i in range(BANK_SLOTS):
+                    b_cols = slice((first + i) * P, (first + i + 1) * P)
+                    for g in range(PASSES2):
+                        nc.tensor.matmul_mx(
+                            out=o_acc[c, first][:, i, :],
+                            lhsT=h_codes[c][:, g, b_cols].bitcast(FP8X4),
+                            lhsT_scale=h_scales[c][:, g, b_cols],
+                            rhs=w2_codes[:, g, :].bitcast(FP8X4),
+                            rhs_scale=w2_scales[:, g, :],
+                            start=(g == 0),
+                            stop=(g == PASSES2 - 1),
+                        )
 
         def add_b2_and_store(c):
             slots = slice(c * CHUNK_SLOTS, (c + 1) * CHUNK_SLOTS)
             mean_std[c] = work.tile([P, 2, CHUNK_SLOTS, LATENT], F32, name="mean_std")
-            nc.vector.tensor_tensor(
-                out=mean_std[c][:].rearrange("p half i c -> p i half c"),
-                in0=o_acc[c][:].rearrange("p i (half c) -> p i half c", half=2),
-                in1=b2_all[:]
-                .rearrange("p (half c) -> p half c", half=2)
-                .unsqueeze(1)
-                .to_broadcast([P, CHUNK_SLOTS, 2, LATENT]),
-                op=ALU.add,
-            )
+            for first in range(0, CHUNK_SLOTS, BANK_SLOTS):
+                nc.vector.tensor_tensor(
+                    out=mean_std[c][:, :, first : first + BANK_SLOTS, :].rearrange(
+                        "p half i c -> p i half c"
+                    ),
+                    in0=o_acc[c, first][:].rearrange("p i (half c) -> p i half c", half=2),
+                    in1=b2_all[:]
+                    .rearrange("p (half c) -> p half c", half=2)
+                    .unsqueeze(1)
+                    .to_broadcast([P, BANK_SLOTS, 2, LATENT]),
+                    op=ALU.add,
+                )
             nc.sync.dma_start(out=mean_view[:, slots, :], in_=mean_std[c][:, 0])
             nc.sync.dma_start(out=std_view[:, slots, :], in_=mean_std[c][:, 1])
 
@@ -271,28 +291,30 @@ def tile_rssm_pa_t_kernel(
             return 0 <= c < CHUNKS
 
         transpose_x(0)
-        transpose_x(1)
         quantise_w1(0)
         copy_x(0)
         quantise_x(0)
+        transpose_x(1)
         quantise_w1(1)
         copy_x(1)
         quantise_x(1)
         layer1(0, 0)
         transpose_x(2)
         quantise_w2_and_spread_b2()
-        for n in range(CHUNKS + 4):
+        for n in range(CHUNKS + 3):
             if exists(n):
                 layer1(n, 1)
                 regroup_h(n, 0)
-            if exists(n - 4):
-                add_mean_and_store(n - 4)
+            if exists(n - 1):
+                layer2(n - 1)
+            if exists(n - 3):
+                add_mean_and_store(n - 3)
             if exists(n + 2):
                 copy_x(n + 2)
+            if exists(n - 1):
+                add_b2_and_store(n - 1)
             if exists(n - 2):
-                add_b2_and_store(n - 2)
-            if exists(n - 3):
-                root_of_std(n - 3)
+                root_of_std(n - 2)
             if exists(n):
                 regroup_h(n, 1)
             if exists(n + 1):
@@ -301,9 +323,7 @@ def tile_rssm_pa_t_kernel(
                 quantise_x(n + 2)
             if exists(n + 3):
                 transpose_x(n + 3)
-            if exists(n - 3):
-                noise(n - 3)
-            if exists(n - 1):
-                layer2(n - 1)
+            if exists(n - 2):
+                noise(n - 2)
             if exists(n):
                 quantise_h(n)

@@ -90,8 +90,8 @@ def tile_rssm_pa_t_kernel(
             eps_rows[c] = inputs.tile([P, CHUNK_SLOTS, LATENT], BF16, name="eps_rows")
             nc.sync.dma_start(out=eps_rows[c][:], in_=eps_view[:, slots, :])
 
-        load_w1(0)
         load_x(0)
+        load_w1(0)
         nc.sync.dma_start(out=b1[:], in_=rep_b1.rearrange("(g m t) -> m g t", g=PASSES2, t=PACK))
         load_w1(1)
         load_x(1)

@@ -26,10 +26,11 @@ OUT = 2 * LATENT
 
 PASSES2 = HIDDEN // K_PASS
 SLOTS = BATCH // P
-CHUNK_SLOTS = 4
 BANK_SLOTS = 2
-CHUNK_ROWS = CHUNK_SLOTS * P
-CHUNKS = SLOTS // CHUNK_SLOTS
+BANK_COLS = 512
+SIZES = [4] * 8
+CHUNKS = len(SIZES)
+FIRST = [sum(SIZES[:c]) for c in range(CHUNKS)]
 WORD_HALVES = 2
 
 FLOPS = 2 * BATCH * K1 * HIDDEN + 2 * BATCH * HIDDEN * OUT
@@ -77,8 +78,8 @@ def tile_rssm_pa_t_kernel(
             nc.sync.dma_start(out=w1_rows[:, :, h_cols], in_=w1_view[:, :, h_cols])
 
         def load_x(c):
-            slots = slice(c * CHUNK_SLOTS, (c + 1) * CHUNK_SLOTS)
-            x_rows[c] = inputs.tile([P, CHUNK_SLOTS, K1], BF16, name="x_rows")
+            slots = slice(FIRST[c], FIRST[c] + SIZES[c])
+            x_rows[c] = inputs.tile([P, SIZES[c], K1], BF16, name="x_rows")
             nc.sync.dma_start(out=x_rows[c][:, :, 0:STATE], in_=state_view[:, slots, :])
             nc.sync.dma_start(
                 out=x_rows[c][:, :, STATE : STATE + ACTION], in_=action_view[:, slots, :]
@@ -86,8 +87,8 @@ def tile_rssm_pa_t_kernel(
             nc.sync.dma_start(out=x_rows[c][:, :, STATE + ACTION : K1], in_=obs_view[:, slots, :])
 
         def load_eps(c):
-            slots = slice(c * CHUNK_SLOTS, (c + 1) * CHUNK_SLOTS)
-            eps_rows[c] = inputs.tile([P, CHUNK_SLOTS, LATENT], BF16, name="eps_rows")
+            slots = slice(FIRST[c], FIRST[c] + SIZES[c])
+            eps_rows[c] = inputs.tile([P, SIZES[c], LATENT], BF16, name="eps_rows")
             nc.sync.dma_start(out=eps_rows[c][:], in_=eps_view[:, slots, :])
 
         load_x(0)
@@ -165,7 +166,7 @@ def tile_rssm_pa_t_kernel(
 
         def transpose_x(c):
             x_words = x_rows[c][:].bitcast(F32).rearrange("p i (q u) -> p i u q", u=WORD_HALVES)
-            for first in range(0, CHUNK_SLOTS, BANK_SLOTS):
+            for first in range(0, SIZES[c], BANK_SLOTS):
                 x_t[c, first] = psum_x.tile([P, BANK_SLOTS, WORD_HALVES, P], F32, name="x_t")
                 for i in range(BANK_SLOTS):
                     for u in range(WORD_HALVES):
@@ -175,33 +176,33 @@ def tile_rssm_pa_t_kernel(
 
         def copy_x(c):
             x_grouped[c] = work.tile(
-                [P, CHUNK_ROWS * PACK], BF16, align_bytes=64, name="x_grouped"
+                [P, SIZES[c] * P * PACK], BF16, align_bytes=64, name="x_grouped"
             )
             x_grouped_words = (
                 x_grouped[c][:]
                 .bitcast(F32)
-                .rearrange("q (i b u) -> q i b u", i=CHUNK_SLOTS, u=WORD_HALVES)
+                .rearrange("q (i b u) -> q i b u", i=SIZES[c], u=WORD_HALVES)
             )
-            for first in range(0, CHUNK_SLOTS, BANK_SLOTS):
+            for first in range(0, SIZES[c], BANK_SLOTS):
                 nc.scalar.copy(
                     out=x_grouped_words[:, first : first + BANK_SLOTS],
                     in_=x_t[c, first][:].rearrange("q i u b -> q i b u"),
                 )
 
         def quantise_x(c):
-            x_codes[c] = work.tile([P, CHUNK_ROWS], U32, align_bytes=64, name="x_codes")
-            x_scales[c] = work.tile([P, CHUNK_ROWS], U8, align_bytes=64, name="x_scales")
+            x_codes[c] = work.tile([P, SIZES[c] * P], U32, align_bytes=64, name="x_codes")
+            x_scales[c] = work.tile([P, SIZES[c] * P], U8, align_bytes=64, name="x_scales")
             nc.vector.quantize_mx(
                 out=x_codes[c][:].bitcast(FP8X4), scales=x_scales[c][:], in_=x_grouped[c][:]
             )
 
         def layer1(c, g):
-            h_tiles[c, g] = work.tile([P, PACK, CHUNK_ROWS], BF16, name="h_tiles")
+            h_tiles[c, g] = work.tile([P, PACK, SIZES[c] * P], BF16, name="h_tiles")
             for t in range(PACK):
                 m_cols = slice((g * PACK + t) * P, (g * PACK + t + 1) * P)
-                h_acc = psum_h.tile([P, CHUNK_ROWS], F32)
+                h_acc = psum_h.tile([P, BANK_COLS], F32)
                 nc.tensor.matmul_mx(
-                    out=h_acc[:],
+                    out=h_acc[:, 0 : SIZES[c] * P],
                     lhsT=w1_codes[:, m_cols].bitcast(FP8X4),
                     lhsT_scale=w1_scales[:, m_cols],
                     rhs=x_codes[c][:].bitcast(FP8X4),
@@ -211,7 +212,7 @@ def tile_rssm_pa_t_kernel(
                 )
                 nc.scalar.activation(
                     out=h_tiles[c, g][:, t, :],
-                    in_=h_acc[:],
+                    in_=h_acc[:, 0 : SIZES[c] * P],
                     func=ACT.Relu,
                     bias=b1[:, g, t : t + 1],
                     scale=1.0,
@@ -220,7 +221,7 @@ def tile_rssm_pa_t_kernel(
         def regroup_h(c, g):
             if g == 0:
                 h_grouped[c] = work.tile(
-                    [P, PASSES2, CHUNK_ROWS, PACK], BF16, align_bytes=64, name="h_grouped"
+                    [P, PASSES2, SIZES[c] * P, PACK], BF16, align_bytes=64, name="h_grouped"
                 )
             nc.vector.tensor_copy(
                 out=h_grouped[c][:, g].rearrange("m (r n) t -> m r t n", n=4),
@@ -228,8 +229,8 @@ def tile_rssm_pa_t_kernel(
             )
 
         def quantise_h(c):
-            h_codes[c] = work.tile([P, PASSES2, CHUNK_ROWS], U32, align_bytes=64, name="h_codes")
-            h_scales[c] = work.tile([P, PASSES2, CHUNK_ROWS], U8, align_bytes=64, name="h_scales")
+            h_codes[c] = work.tile([P, PASSES2, SIZES[c] * P], U32, align_bytes=64, name="h_codes")
+            h_scales[c] = work.tile([P, PASSES2, SIZES[c] * P], U8, align_bytes=64, name="h_scales")
             nc.vector.quantize_mx(
                 out=h_codes[c][:].rearrange("m g b -> m (g b)").bitcast(FP8X4),
                 scales=h_scales[c][:].rearrange("m g b -> m (g b)"),
@@ -237,7 +238,7 @@ def tile_rssm_pa_t_kernel(
             )
 
         def layer2(c):
-            for first in range(0, CHUNK_SLOTS, BANK_SLOTS):
+            for first in range(0, SIZES[c], BANK_SLOTS):
                 o_acc[c, first] = psum_o.tile([P, BANK_SLOTS, OUT], F32, name="o_acc")
                 for i in range(BANK_SLOTS):
                     b_cols = slice((first + i) * P, (first + i + 1) * P)
@@ -253,9 +254,9 @@ def tile_rssm_pa_t_kernel(
                         )
 
         def add_b2_and_store(c):
-            slots = slice(c * CHUNK_SLOTS, (c + 1) * CHUNK_SLOTS)
-            mean_std[c] = work.tile([P, 2, CHUNK_SLOTS, LATENT], F32, name="mean_std")
-            for first in range(0, CHUNK_SLOTS, BANK_SLOTS):
+            slots = slice(FIRST[c], FIRST[c] + SIZES[c])
+            mean_std[c] = work.tile([P, 2, SIZES[c], LATENT], F32, name="mean_std")
+            for first in range(0, SIZES[c], BANK_SLOTS):
                 nc.vector.tensor_tensor(
                     out=mean_std[c][:, :, first : first + BANK_SLOTS, :].rearrange(
                         "p half i c -> p i half c"
@@ -271,17 +272,17 @@ def tile_rssm_pa_t_kernel(
             nc.sync.dma_start(out=std_view[:, slots, :], in_=mean_std[c][:, 1])
 
         def root_of_std(c):
-            root[c] = work.tile([P, CHUNK_SLOTS, LATENT], F32, name="root")
+            root[c] = work.tile([P, SIZES[c], LATENT], F32, name="root")
             nc.scalar.activation(out=root[c][:], in_=mean_std[c][:, 1], func=ACT.Sqrt)
 
         def noise(c):
-            sample[c] = work.tile([P, CHUNK_SLOTS, LATENT], F32, name="sample")
+            sample[c] = work.tile([P, SIZES[c], LATENT], F32, name="sample")
             nc.vector.tensor_tensor(
                 out=sample[c][:], in0=root[c][:], in1=eps_rows[c][:], op=ALU.mult
             )
 
         def add_mean_and_store(c):
-            slots = slice(c * CHUNK_SLOTS, (c + 1) * CHUNK_SLOTS)
+            slots = slice(FIRST[c], FIRST[c] + SIZES[c])
             nc.vector.tensor_tensor(
                 out=sample[c][:], in0=sample[c][:], in1=mean_std[c][:, 0], op=ALU.add
             )
@@ -294,25 +295,26 @@ def tile_rssm_pa_t_kernel(
         quantise_w1(0)
         copy_x(0)
         quantise_x(0)
-        transpose_x(1)
-        quantise_w1(1)
-        copy_x(1)
-        quantise_x(1)
         layer1(0, 0)
-        transpose_x(2)
+        quantise_w1(1)
+        transpose_x(1)
+        copy_x(1)
+        regroup_h(0, 0)
+        quantise_x(1)
         quantise_w2_and_spread_b2()
         for n in range(CHUNKS + 3):
             if exists(n):
                 layer1(n, 1)
-                regroup_h(n, 0)
             if exists(n - 1):
                 layer2(n - 1)
             if exists(n - 3):
                 add_mean_and_store(n - 3)
             if exists(n + 2):
-                copy_x(n + 2)
+                transpose_x(n + 2)
             if exists(n - 1):
                 add_b2_and_store(n - 1)
+            if exists(n + 2):
+                copy_x(n + 2)
             if exists(n - 2):
                 root_of_std(n - 2)
             if exists(n):
@@ -321,9 +323,9 @@ def tile_rssm_pa_t_kernel(
                 layer1(n + 1, 0)
             if exists(n + 2):
                 quantise_x(n + 2)
-            if exists(n + 3):
-                transpose_x(n + 3)
             if exists(n - 2):
                 noise(n - 2)
             if exists(n):
                 quantise_h(n)
+            if exists(n + 1):
+                regroup_h(n + 1, 0)

@@ -28,7 +28,7 @@ PASSES2 = HIDDEN // K_PASS
 SLOTS = BATCH // P
 BANK_SLOTS = 2
 BANK_COLS = 512
-SIZES = [4] * 8
+SIZES = [4, 4, 4, 4, 4, 4, 4, 2, 2]
 CHUNKS = len(SIZES)
 FIRST = [sum(SIZES[:c]) for c in range(CHUNKS)]
 WORD_HALVES = 2
@@ -92,14 +92,14 @@ def tile_rssm_pa_t_kernel(
             nc.sync.dma_start(out=eps_rows[c][:], in_=eps_view[:, slots, :])
 
         load_x(0)
-        load_w1(0)
         nc.sync.dma_start(out=b1[:], in_=rep_b1.rearrange("(g m t) -> m g t", g=PASSES2, t=PACK))
-        load_w1(1)
+        load_w1(0)
+        nc.sync.dma_start(out=b2_row[0:1, :], in_=rep_b2.rearrange("(o c) -> o c", o=1))
         load_x(1)
+        load_w1(1)
         nc.sync.dma_start(
             out=w2_rows[:], in_=rep_W2.rearrange("(g p j) c -> p g j c", g=PASSES2, j=PACK)
         )
-        nc.sync.dma_start(out=b2_row[0:1, :], in_=rep_b2.rearrange("(o c) -> o c", o=1))
         for c in range(2, CHUNKS):
             load_x(c)
             load_eps(c - 2)
@@ -126,30 +126,35 @@ def tile_rssm_pa_t_kernel(
         w2_scales = keep.tile([P, PASSES2, OUT], U8, align_bytes=64)
         b2_all = keep.tile([P, OUT], F32)
 
-        def quantise_w1(g):
+        def regroup_w1(g):
             h_cols = slice(g * K_PASS, (g + 1) * K_PASS)
             nc.vector.tensor_copy(
                 out=w1_grouped[:, h_cols, :].rearrange("p (t m) j -> p t m j", t=PACK),
                 in_=w1_rows[:, :, h_cols].rearrange("p j (m t) -> p t m j", t=PACK),
             )
+
+        def quantise_w1(g):
+            h_cols = slice(g * K_PASS, (g + 1) * K_PASS)
             nc.vector.quantize_mx(
                 out=w1_codes[:, h_cols].bitcast(FP8X4),
                 scales=w1_scales[:, h_cols],
                 in_=w1_grouped[:, h_cols, :].rearrange("p h j -> p (h j)"),
             )
 
-        def quantise_w2_and_spread_b2():
+        def quantise_w2():
             nc.vector.tensor_copy(
                 out=w2_grouped[:], in_=w2_rows[:].rearrange("p g j c -> p g c j")
             )
-            b2_acc = psum_o.tile([P, BANK_SLOTS, OUT], F32, name="o_acc")
-            nc.tensor.matmul(out=b2_acc[:, 0, :], lhsT=ones[:], rhs=b2_row[:], start=True, stop=True)
-            nc.vector.tensor_copy(out=b2_all[:], in_=b2_acc[:, 0, :])
             nc.vector.quantize_mx(
                 out=w2_codes[:].rearrange("p g c -> p (g c)").bitcast(FP8X4),
                 scales=w2_scales[:].rearrange("p g c -> p (g c)"),
                 in_=w2_grouped[:].rearrange("p g c j -> p (g c j)"),
             )
+
+        def spread_b2():
+            b2_acc = psum_o.tile([P, BANK_SLOTS, OUT], F32, name="o_acc")
+            nc.tensor.matmul(out=b2_acc[:, 0, :], lhsT=ones[:], rhs=b2_row[:], start=True, stop=True)
+            nc.scalar.copy(out=b2_all[:], in_=b2_acc[:, 0, :])
 
         x_t = {}
         x_grouped = {}
@@ -283,7 +288,7 @@ def tile_rssm_pa_t_kernel(
 
         def add_mean_and_store(c):
             slots = slice(FIRST[c], FIRST[c] + SIZES[c])
-            nc.vector.tensor_tensor(
+            nc.gpsimd.tensor_tensor(
                 out=sample[c][:], in0=sample[c][:], in1=mean_std[c][:, 0], op=ALU.add
             )
             nc.sync.dma_start(out=sample_view[:, slots, :], in_=sample[c][:])
@@ -291,41 +296,46 @@ def tile_rssm_pa_t_kernel(
         def exists(c):
             return 0 <= c < CHUNKS
 
+        regroup_w1(0)
         transpose_x(0)
-        quantise_w1(0)
         copy_x(0)
         quantise_x(0)
-        layer1(0, 0)
-        quantise_w1(1)
         transpose_x(1)
+        quantise_w1(0)
+        regroup_w1(1)
         copy_x(1)
-        regroup_h(0, 0)
+        spread_b2()
+        quantise_w1(1)
+        layer1(0, 0)
+        quantise_w2()
         quantise_x(1)
-        quantise_w2_and_spread_b2()
+        transpose_x(2)
+        regroup_h(0, 0)
+        copy_x(2)
         for n in range(CHUNKS + 3):
             if exists(n):
                 layer1(n, 1)
+            if exists(n + 3):
+                transpose_x(n + 3)
+            if exists(n + 2):
+                quantise_x(n + 2)
+            if exists(n - 3):
+                root_of_std(n - 3)
+            if exists(n - 2):
+                add_b2_and_store(n - 2)
+            if exists(n):
+                regroup_h(n, 1)
+            if exists(n - 3):
+                noise(n - 3)
+            if exists(n + 1):
+                layer1(n + 1, 0)
+            if exists(n):
+                quantise_h(n)
             if exists(n - 1):
                 layer2(n - 1)
             if exists(n - 3):
                 add_mean_and_store(n - 3)
-            if exists(n + 2):
-                transpose_x(n + 2)
-            if exists(n - 1):
-                add_b2_and_store(n - 1)
-            if exists(n + 2):
-                copy_x(n + 2)
-            if exists(n - 2):
-                root_of_std(n - 2)
-            if exists(n):
-                regroup_h(n, 1)
-            if exists(n + 1):
-                layer1(n + 1, 0)
-            if exists(n + 2):
-                quantise_x(n + 2)
-            if exists(n - 2):
-                noise(n - 2)
-            if exists(n):
-                quantise_h(n)
             if exists(n + 1):
                 regroup_h(n + 1, 0)
+            if exists(n + 3):
+                copy_x(n + 3)

@@ -92,11 +92,11 @@ def tile_rssm_pa_t_kernel(
             nc.sync.dma_start(out=eps_rows[c][:], in_=eps_view[:, slots, :])
 
         load_x(0)
-        nc.sync.dma_start(out=b1[:], in_=rep_b1.rearrange("(g m t) -> m g t", g=PASSES2, t=PACK))
         load_w1(0)
-        nc.sync.dma_start(out=b2_row[0:1, :], in_=rep_b2.rearrange("(o c) -> o c", o=1))
+        nc.sync.dma_start(out=b1[:], in_=rep_b1.rearrange("(g m t) -> m g t", g=PASSES2, t=PACK))
         load_x(1)
         load_w1(1)
+        nc.sync.dma_start(out=b2_row[0:1, :], in_=rep_b2.rearrange("(o c) -> o c", o=1))
         nc.sync.dma_start(
             out=w2_rows[:], in_=rep_W2.rearrange("(g p j) c -> p g j c", g=PASSES2, j=PACK)
         )
@@ -141,10 +141,12 @@ def tile_rssm_pa_t_kernel(
                 in_=w1_grouped[:, h_cols, :].rearrange("p h j -> p (h j)"),
             )
 
-        def quantise_w2():
+        def regroup_w2():
             nc.vector.tensor_copy(
                 out=w2_grouped[:], in_=w2_rows[:].rearrange("p g j c -> p g c j")
             )
+
+        def quantise_w2():
             nc.vector.quantize_mx(
                 out=w2_codes[:].rearrange("p g c -> p (g c)").bitcast(FP8X4),
                 scales=w2_scales[:].rearrange("p g c -> p (g c)"),
@@ -296,46 +298,43 @@ def tile_rssm_pa_t_kernel(
         def exists(c):
             return 0 <= c < CHUNKS
 
-        regroup_w1(0)
         transpose_x(0)
+        regroup_w1(0)
         copy_x(0)
         quantise_x(0)
-        transpose_x(1)
         quantise_w1(0)
         regroup_w1(1)
+        quantise_w1(1)
+        regroup_w2()
+        transpose_x(1)
         copy_x(1)
         spread_b2()
-        quantise_w1(1)
         layer1(0, 0)
+        layer1(0, 1)
         quantise_w2()
-        quantise_x(1)
-        transpose_x(2)
-        regroup_h(0, 0)
-        copy_x(2)
-        for n in range(CHUNKS + 3):
-            if exists(n):
-                layer1(n, 1)
+        for n in range(-1, CHUNKS + 3):
             if exists(n + 3):
                 transpose_x(n + 3)
-            if exists(n + 2):
-                quantise_x(n + 2)
-            if exists(n - 3):
-                root_of_std(n - 3)
-            if exists(n - 2):
-                add_b2_and_store(n - 2)
             if exists(n):
+                regroup_h(n, 0)
                 regroup_h(n, 1)
             if exists(n - 3):
                 noise(n - 3)
-            if exists(n + 1):
-                layer1(n + 1, 0)
             if exists(n):
                 quantise_h(n)
-            if exists(n - 1):
-                layer2(n - 1)
+            if exists(n + 2):
+                quantise_x(n + 2)
             if exists(n - 3):
                 add_mean_and_store(n - 3)
-            if exists(n + 1):
-                regroup_h(n + 1, 0)
             if exists(n + 3):
                 copy_x(n + 3)
+            if exists(n + 2):
+                layer1(n + 2, 0)
+            if exists(n - 1):
+                add_b2_and_store(n - 1)
+            if exists(n):
+                layer2(n)
+            if exists(n + 2):
+                layer1(n + 2, 1)
+            if exists(n - 1):
+                root_of_std(n - 1)

@@ -91,12 +91,12 @@ def tile_rssm_pa_t_kernel(
             eps_rows[c] = inputs.tile([P, SIZES[c], LATENT], BF16, name="eps_rows")
             nc.sync.dma_start(out=eps_rows[c][:], in_=eps_view[:, slots, :])
 
-        load_x(0)
         load_w1(0)
-        nc.sync.dma_start(out=b1[:], in_=rep_b1.rearrange("(g m t) -> m g t", g=PASSES2, t=PACK))
-        load_x(1)
+        load_x(0)
         load_w1(1)
         nc.sync.dma_start(out=b2_row[0:1, :], in_=rep_b2.rearrange("(o c) -> o c", o=1))
+        load_x(1)
+        nc.sync.dma_start(out=b1[:], in_=rep_b1.rearrange("(g m t) -> m g t", g=PASSES2, t=PACK))
         nc.sync.dma_start(
             out=w2_rows[:], in_=rep_W2.rearrange("(g p j) c -> p g j c", g=PASSES2, j=PACK)
         )
@@ -290,51 +290,52 @@ def tile_rssm_pa_t_kernel(
 
         def add_mean_and_store(c):
             slots = slice(FIRST[c], FIRST[c] + SIZES[c])
-            nc.gpsimd.tensor_tensor(
-                out=sample[c][:], in0=sample[c][:], in1=mean_std[c][:, 0], op=ALU.add
-            )
+            add = nc.vector.tensor_tensor if c == CHUNKS - 1 else nc.gpsimd.tensor_tensor
+            add(out=sample[c][:], in0=sample[c][:], in1=mean_std[c][:, 0], op=ALU.add)
             nc.sync.dma_start(out=sample_view[:, slots, :], in_=sample[c][:])
 
         def exists(c):
             return 0 <= c < CHUNKS
 
-        transpose_x(0)
         regroup_w1(0)
+        transpose_x(0)
         copy_x(0)
-        quantise_x(0)
-        quantise_w1(0)
-        regroup_w1(1)
-        quantise_w1(1)
-        regroup_w2()
-        transpose_x(1)
-        copy_x(1)
         spread_b2()
+        transpose_x(1)
+        quantise_w1(0)
+        quantise_x(0)
+        copy_x(1)
+        quantise_x(1)
         layer1(0, 0)
+        regroup_w1(1)
+        layer1(1, 0)
+        quantise_w1(1)
         layer1(0, 1)
+        regroup_w2()
+        transpose_x(2)
+        copy_x(2)
         quantise_w2()
-        for n in range(-1, CHUNKS + 3):
-            if exists(n + 3):
-                transpose_x(n + 3)
+        for n in range(CHUNKS + 3):
+            if exists(n - 1):
+                quantise_h(n - 1)
+            if exists(n - 2):
+                add_b2_and_store(n - 2)
+            if exists(n - 1):
+                layer2(n - 1)
             if exists(n):
                 regroup_h(n, 0)
                 regroup_h(n, 1)
-            if exists(n - 3):
-                noise(n - 3)
-            if exists(n):
-                quantise_h(n)
             if exists(n + 2):
                 quantise_x(n + 2)
+            if exists(n + 1):
+                layer1(n + 1, 1)
             if exists(n - 3):
+                noise(n - 3)
                 add_mean_and_store(n - 3)
             if exists(n + 3):
+                transpose_x(n + 3)
                 copy_x(n + 3)
+            if exists(n - 2):
+                root_of_std(n - 2)
             if exists(n + 2):
                 layer1(n + 2, 0)
-            if exists(n - 1):
-                add_b2_and_store(n - 1)
-            if exists(n):
-                layer2(n)
-            if exists(n + 2):
-                layer1(n + 2, 1)
-            if exists(n - 1):
-                root_of_std(n - 1)

from contextlib import ExitStack

import concourse.mybir as mybir
from concourse.masks import make_identity

F32 = mybir.dt.float32
BF16 = mybir.dt.bfloat16
U32 = mybir.dt.uint32
U8 = mybir.dt.uint8
FP8X4 = mybir.dt.float8_e4m3fn_x4
ACT = mybir.ActivationFunctionType
ALU = mybir.AluOpType

P = 128
PACK = 4
K_PASS = P * PACK

BATCH = 4096
STATE = 256
ACTION = 128
OBS = 128
K1 = STATE + ACTION + OBS
HIDDEN = 1024
LATENT = 128
OUT = 2 * LATENT

PASSES2 = HIDDEN // K_PASS
SLOTS = BATCH // P
BANK_SLOTS = 2
BANK_COLS = 512
SIZES = [4, 4, 4, 4, 4, 4, 4, 2, 2]
CHUNKS = len(SIZES)
FIRST = [sum(SIZES[:c]) for c in range(CHUNKS)]
WORD_HALVES = 2

FLOPS = 2 * BATCH * K1 * HIDDEN + 2 * BATCH * HIDDEN * OUT


def tile_rssm_pa_t_kernel(
    tc,
    prev_state,
    prev_action,
    observation,
    eps,
    rep_W1,
    rep_b1,
    rep_W2,
    rep_b2,
    mean_out,
    std_out,
    sample_out,
):
    nc = tc.nc
    with ExitStack() as stack:
        stack.enter_context(tc.manual_schedule())
        keep = stack.enter_context(tc.tile_pool(name="keep", bufs=1))
        inputs = stack.enter_context(tc.tile_pool(name="inputs", bufs=CHUNKS))
        work = stack.enter_context(tc.tile_pool(name="work", bufs=4))
        psum_x = stack.enter_context(tc.psum_pool(name="psum_x", bufs=2))
        psum_h = stack.enter_context(tc.psum_pool(name="psum_h", bufs=4))
        psum_o = stack.enter_context(tc.psum_pool(name="psum_o", bufs=2))

        w1_rows = keep.tile([P, PACK, HIDDEN], BF16)
        w1_view = rep_W1.rearrange("(p j) h -> p j h", j=PACK)
        b1 = keep.tile([P, PASSES2, PACK], BF16)
        w2_rows = keep.tile([P, PASSES2, PACK, OUT], BF16)
        b2_row = keep.tile([P, OUT], BF16)
        nc.vector.memset(b2_row[:], 0.0)
        state_view = prev_state.rearrange("(p i) k -> p i k", i=SLOTS)
        action_view = prev_action.rearrange("(p i) k -> p i k", i=SLOTS)
        obs_view = observation.rearrange("(p i) k -> p i k", i=SLOTS)
        eps_view = eps.rearrange("(p i) c -> p i c", i=SLOTS)
        x_rows = {}
        eps_rows = {}

        def load_w1(g):
            h_cols = slice(g * K_PASS, (g + 1) * K_PASS)
            nc.sync.dma_start(out=w1_rows[:, :, h_cols], in_=w1_view[:, :, h_cols])

        def load_x(c):
            slots = slice(FIRST[c], FIRST[c] + SIZES[c])
            x_rows[c] = inputs.tile([P, SIZES[c], K1], BF16, name="x_rows")
            nc.sync.dma_start(out=x_rows[c][:, :, 0:STATE], in_=state_view[:, slots, :])
            nc.sync.dma_start(
                out=x_rows[c][:, :, STATE : STATE + ACTION], in_=action_view[:, slots, :]
            )
            nc.sync.dma_start(out=x_rows[c][:, :, STATE + ACTION : K1], in_=obs_view[:, slots, :])

        def load_eps(c):
            slots = slice(FIRST[c], FIRST[c] + SIZES[c])
            eps_rows[c] = inputs.tile([P, SIZES[c], LATENT], BF16, name="eps_rows")
            nc.sync.dma_start(out=eps_rows[c][:], in_=eps_view[:, slots, :])

        load_w1(0)
        load_x(0)
        load_w1(1)
        nc.sync.dma_start(out=b2_row[0:1, :], in_=rep_b2.rearrange("(o c) -> o c", o=1))
        load_x(1)
        nc.sync.dma_start(out=b1[:], in_=rep_b1.rearrange("(g m t) -> m g t", g=PASSES2, t=PACK))
        nc.sync.dma_start(
            out=w2_rows[:], in_=rep_W2.rearrange("(g p j) c -> p g j c", g=PASSES2, j=PACK)
        )
        for c in range(2, CHUNKS):
            load_x(c)
            load_eps(c - 2)
        load_eps(CHUNKS - 2)
        load_eps(CHUNKS - 1)

        mean_view = mean_out.rearrange("(p i) c -> p i c", i=SLOTS)
        std_view = std_out.rearrange("(p i) c -> p i c", i=SLOTS)
        sample_view = sample_out.rearrange("(p i) c -> p i c", i=SLOTS)

        identity = keep.tile([P, P], F32)
        make_identity(nc, identity[:])
        ones = keep.tile([P, P], BF16)
        nc.vector.memset(ones[:], 1.0)
        one = keep.tile([P, 1], F32)
        nc.vector.memset(one[:], 1.0)
        nc.scalar.activation(out=one[:], in_=one[:], func=ACT.Sqrt)

        w1_grouped = keep.tile([P, HIDDEN, PACK], BF16, align_bytes=64)
        w1_codes = keep.tile([P, HIDDEN], U32, align_bytes=64)
        w1_scales = keep.tile([P, HIDDEN], U8, align_bytes=64)
        w2_grouped = keep.tile([P, PASSES2, OUT, PACK], BF16, align_bytes=64)
        w2_codes = keep.tile([P, PASSES2, OUT], U32, align_bytes=64)
        w2_scales = keep.tile([P, PASSES2, OUT], U8, align_bytes=64)
        b2_all = keep.tile([P, OUT], F32)

        def regroup_w1(g):
            h_cols = slice(g * K_PASS, (g + 1) * K_PASS)
            nc.vector.tensor_copy(
                out=w1_grouped[:, h_cols, :].rearrange("p (t m) j -> p t m j", t=PACK),
                in_=w1_rows[:, :, h_cols].rearrange("p j (m t) -> p t m j", t=PACK),
            )

        def quantise_w1(g):
            h_cols = slice(g * K_PASS, (g + 1) * K_PASS)
            nc.vector.quantize_mx(
                out=w1_codes[:, h_cols].bitcast(FP8X4),
                scales=w1_scales[:, h_cols],
                in_=w1_grouped[:, h_cols, :].rearrange("p h j -> p (h j)"),
            )

        def regroup_w2():
            nc.vector.tensor_copy(
                out=w2_grouped[:], in_=w2_rows[:].rearrange("p g j c -> p g c j")
            )

        def quantise_w2():
            nc.vector.quantize_mx(
                out=w2_codes[:].rearrange("p g c -> p (g c)").bitcast(FP8X4),
                scales=w2_scales[:].rearrange("p g c -> p (g c)"),
                in_=w2_grouped[:].rearrange("p g c j -> p (g c j)"),
            )

        def spread_b2():
            b2_acc = psum_o.tile([P, BANK_SLOTS, OUT], F32, name="o_acc")
            nc.tensor.matmul(out=b2_acc[:, 0, :], lhsT=ones[:], rhs=b2_row[:], start=True, stop=True)
            nc.scalar.copy(out=b2_all[:], in_=b2_acc[:, 0, :])

        x_t = {}
        x_grouped = {}
        x_codes = {}
        x_scales = {}
        h_tiles = {}
        h_grouped = {}
        h_codes = {}
        h_scales = {}
        o_acc = {}
        mean_std = {}
        root = {}
        sample = {}

        def transpose_x(c):
            x_words = x_rows[c][:].bitcast(F32).rearrange("p i (q u) -> p i u q", u=WORD_HALVES)
            for first in range(0, SIZES[c], BANK_SLOTS):
                x_t[c, first] = psum_x.tile([P, BANK_SLOTS, WORD_HALVES, P], F32, name="x_t")
                for i in range(BANK_SLOTS):
                    for u in range(WORD_HALVES):
                        nc.tensor.transpose(
                            x_t[c, first][:, i, u, :], x_words[:, first + i, u, :], identity[:]
                        )

        def copy_x(c):
            x_grouped[c] = work.tile(
                [P, SIZES[c] * P * PACK], BF16, align_bytes=64, name="x_grouped"
            )
            x_grouped_words = (
                x_grouped[c][:]
                .bitcast(F32)
                .rearrange("q (i b u) -> q i b u", i=SIZES[c], u=WORD_HALVES)
            )
            for first in range(0, SIZES[c], BANK_SLOTS):
                nc.scalar.copy(
                    out=x_grouped_words[:, first : first + BANK_SLOTS],
                    in_=x_t[c, first][:].rearrange("q i u b -> q i b u"),
                )

        def quantise_x(c):
            x_codes[c] = work.tile([P, SIZES[c] * P], U32, align_bytes=64, name="x_codes")
            x_scales[c] = work.tile([P, SIZES[c] * P], U8, align_bytes=64, name="x_scales")
            nc.vector.quantize_mx(
                out=x_codes[c][:].bitcast(FP8X4), scales=x_scales[c][:], in_=x_grouped[c][:]
            )

        def layer1(c, g):
            h_tiles[c, g] = work.tile([P, PACK, SIZES[c] * P], BF16, name="h_tiles")
            for t in range(PACK):
                m_cols = slice((g * PACK + t) * P, (g * PACK + t + 1) * P)
                h_acc = psum_h.tile([P, BANK_COLS], F32)
                nc.tensor.matmul_mx(
                    out=h_acc[:, 0 : SIZES[c] * P],
                    lhsT=w1_codes[:, m_cols].bitcast(FP8X4),
                    lhsT_scale=w1_scales[:, m_cols],
                    rhs=x_codes[c][:].bitcast(FP8X4),
                    rhs_scale=x_scales[c][:],
                    start=True,
                    stop=True,
                )
                nc.scalar.activation(
                    out=h_tiles[c, g][:, t, :],
                    in_=h_acc[:, 0 : SIZES[c] * P],
                    func=ACT.Relu,
                    bias=b1[:, g, t : t + 1],
                    scale=1.0,
                )

        def regroup_h(c, g):
            if g == 0:
                h_grouped[c] = work.tile(
                    [P, PASSES2, SIZES[c] * P, PACK], BF16, align_bytes=64, name="h_grouped"
                )
            nc.vector.tensor_copy(
                out=h_grouped[c][:, g].rearrange("m (r n) t -> m r t n", n=4),
                in_=h_tiles[c, g][:].rearrange("m t (r n) -> m r t n", n=4),
            )

        def quantise_h(c):
            h_codes[c] = work.tile([P, PASSES2, SIZES[c] * P], U32, align_bytes=64, name="h_codes")
            h_scales[c] = work.tile([P, PASSES2, SIZES[c] * P], U8, align_bytes=64, name="h_scales")
            nc.vector.quantize_mx(
                out=h_codes[c][:].rearrange("m g b -> m (g b)").bitcast(FP8X4),
                scales=h_scales[c][:].rearrange("m g b -> m (g b)"),
                in_=h_grouped[c][:].rearrange("m g b t -> m (g b t)"),
            )

        def layer2(c):
            for first in range(0, SIZES[c], BANK_SLOTS):
                o_acc[c, first] = psum_o.tile([P, BANK_SLOTS, OUT], F32, name="o_acc")
                for i in range(BANK_SLOTS):
                    b_cols = slice((first + i) * P, (first + i + 1) * P)
                    for g in range(PASSES2):
                        nc.tensor.matmul_mx(
                            out=o_acc[c, first][:, i, :],
                            lhsT=h_codes[c][:, g, b_cols].bitcast(FP8X4),
                            lhsT_scale=h_scales[c][:, g, b_cols],
                            rhs=w2_codes[:, g, :].bitcast(FP8X4),
                            rhs_scale=w2_scales[:, g, :],
                            start=(g == 0),
                            stop=(g == PASSES2 - 1),
                        )

        def add_b2_and_store(c):
            slots = slice(FIRST[c], FIRST[c] + SIZES[c])
            mean_std[c] = work.tile([P, 2, SIZES[c], LATENT], F32, name="mean_std")
            for first in range(0, SIZES[c], BANK_SLOTS):
                nc.vector.tensor_tensor(
                    out=mean_std[c][:, :, first : first + BANK_SLOTS, :].rearrange(
                        "p half i c -> p i half c"
                    ),
                    in0=o_acc[c, first][:].rearrange("p i (half c) -> p i half c", half=2),
                    in1=b2_all[:]
                    .rearrange("p (half c) -> p half c", half=2)
                    .unsqueeze(1)
                    .to_broadcast([P, BANK_SLOTS, 2, LATENT]),
                    op=ALU.add,
                )
            nc.sync.dma_start(out=mean_view[:, slots, :], in_=mean_std[c][:, 0])
            nc.sync.dma_start(out=std_view[:, slots, :], in_=mean_std[c][:, 1])

        def root_of_std(c):
            root[c] = work.tile([P, SIZES[c], LATENT], F32, name="root")
            nc.scalar.activation(out=root[c][:], in_=mean_std[c][:, 1], func=ACT.Sqrt)

        def noise(c):
            sample[c] = work.tile([P, SIZES[c], LATENT], F32, name="sample")
            nc.vector.tensor_tensor(
                out=sample[c][:], in0=root[c][:], in1=eps_rows[c][:], op=ALU.mult
            )

        def add_mean_and_store(c):
            slots = slice(FIRST[c], FIRST[c] + SIZES[c])
            add = nc.vector.tensor_tensor if c == CHUNKS - 1 else nc.gpsimd.tensor_tensor
            add(out=sample[c][:], in0=sample[c][:], in1=mean_std[c][:, 0], op=ALU.add)
            nc.sync.dma_start(out=sample_view[:, slots, :], in_=sample[c][:])

        def exists(c):
            return 0 <= c < CHUNKS

        regroup_w1(0)
        transpose_x(0)
        copy_x(0)
        spread_b2()
        transpose_x(1)
        quantise_w1(0)
        quantise_x(0)
        copy_x(1)
        quantise_x(1)
        layer1(0, 0)
        regroup_w1(1)
        layer1(1, 0)
        quantise_w1(1)
        layer1(0, 1)
        regroup_w2()
        transpose_x(2)
        copy_x(2)
        quantise_w2()
        for n in range(CHUNKS + 3):
            if exists(n - 1):
                quantise_h(n - 1)
            if exists(n - 2):
                add_b2_and_store(n - 2)
            if exists(n - 1):
                layer2(n - 1)
            if exists(n):
                regroup_h(n, 0)
                regroup_h(n, 1)
            if exists(n + 2):
                quantise_x(n + 2)
            if exists(n + 1):
                layer1(n + 1, 1)
            if exists(n - 3):
                noise(n - 3)
                add_mean_and_store(n - 3)
            if exists(n + 3):
                transpose_x(n + 3)
                copy_x(n + 3)
            if exists(n - 2):
                root_of_std(n - 2)
            if exists(n + 2):
                layer1(n + 2, 0)
